import numpy as np
import ml_dtypes


def mxq(x, axis, fmt="e4m3"):
    dtype, down = {"e4m3": (ml_dtypes.float8_e4m3fn, 7), "e5m2": (ml_dtypes.float8_e5m2, 14)}[fmt]
    v = np.moveaxis(np.asarray(x, np.float32).astype(ml_dtypes.bfloat16).astype(np.float64), axis, -1)
    blocks = v.reshape(v.shape[:-1] + (-1, 32))
    amax = np.abs(blocks).max(-1, keepdims=True)
    byte = np.maximum(np.where(amax > 0, np.frexp(amax)[1] - 1 + 127, 0) - down, 1)
    scale = np.exp2(byte - 127.0)
    codes = (blocks / scale).astype(np.float32).astype(dtype).astype(np.float64)
    return np.moveaxis((codes * scale).reshape(v.shape), -1, axis)


WIDE = False


def mx_kscale(k):
    if not WIDE:
        return np.ones(k)
    levels = np.array([10, -10, 5, -5, 0])
    a = np.random.permutation(np.resize(levels, k // 512 * 4)).reshape(k // 512, 4)
    idx = np.arange(k)
    return np.exp2(a[idx // 512, idx % 128 // 32])


BF16 = ml_dtypes.bfloat16


def bf(x):
    return np.asarray(x, np.float32).astype(BF16)


def f64(x):
    return np.asarray(x).astype(np.float64)


B, S, HID, H, QLR, KVLR, DN, DR, DV = 4, 1024, 1024, 4, 1536, 512, 64, 128, 64
EPS = 1e-6
HALF = DR // 2


def rmsnorm(x):
    return x * (1.0 / np.sqrt(np.mean(x * x, axis=-1, keepdims=True) + EPS))


def rope_tables(seq_len):
    inv_freq = 1.0 / (10000.0 ** (np.arange(0, DR, 2) / DR))
    ang = np.arange(seq_len)[:, None] * inv_freq[None, :]
    cos = np.concatenate([np.cos(ang), np.cos(ang)], axis=-1)
    sin = np.concatenate([np.sin(ang), np.sin(ang)], axis=-1)
    return cos, sin


def apply_rope(x, cos, sin):
    rh = np.concatenate([-x[..., HALF:], x[..., :HALF]], axis=-1)
    return x * cos + rh * sin


def setup_inputs():
    s = mx_kscale(HID)
    return {"X": bf(np.random.standard_normal((B, S, HID)) * s),
            "Wkv_down": bf(np.random.standard_normal((HID, DR + KVLR)) / np.sqrt(HID) / s[:, None]),
            "bkv_down": bf(np.random.standard_normal(DR + KVLR) * 0.2),
            "Wkv_up": bf(np.random.standard_normal((KVLR, H * (DN + DV))) / np.sqrt(KVLR)),
            "bkv_up": bf(np.random.standard_normal(H * (DN + DV)) * 0.2)}


def reference(X, Wkv_down, bkv_down, Wkv_up, bkv_up):
    ckv = (mxq(f64(X), 2, "e4m3") @ mxq(f64(Wkv_down), 0, "e4m3")) + f64(bkv_down)
    k_rope = ckv[..., :DR].reshape(B, S, 1, DR).transpose(0, 2, 1, 3)
    kv = (mxq(rmsnorm(ckv[..., DR:]), 2, "e4m3") @ mxq(f64(Wkv_up), 0, "e4m3")) + f64(bkv_up)
    kv = kv.reshape(B, S, H, DN + DV).transpose(0, 2, 1, 3)
    k_nope, value = kv[..., :DN], kv[..., DN:]
    cos, sin = rope_tables(S)
    k_rope = apply_rope(k_rope, cos, sin)
    key = np.concatenate([k_nope, np.broadcast_to(k_rope, (B, H, S, DR))], axis=-1)
    return key, np.ascontiguousarray(value)

@@ -1,0 +1,328 @@
+from contextlib import ExitStack
+import math
+
+import concourse.mybir as mybir
+from concourse.masks import make_identity
+
+FLOPS = 2 * 4096 * (1024 * 640 + 512 * 512)
+
+F32 = mybir.dt.float32
+BF16 = mybir.dt.bfloat16
+U32 = mybir.dt.uint32
+U8 = mybir.dt.uint8
+I32 = mybir.dt.int32
+FP8X4 = mybir.dt.float8_e4m3fn_x4
+AF = mybir.ActivationFunctionType
+ALU = mybir.AluOpType
+
+P = 128
+NQUAD = 8
+NPAIR = 16
+EPS = 1e-6
+TWO_PI = 2.0 * math.pi
+PIN = False
+
+
+def tile_mla_pb_t_kernel(tc, X, Wkv_down, bkv_down, Wkv_up, bkv_up, out_0, out_1):
+    nc = tc.nc
+    with ExitStack() as ctx:
+        const = ctx.enter_context(tc.tile_pool(name="const", bufs=1))
+        xres = ctx.enter_context(tc.tile_pool(name="xres", bufs=6))
+        xg_pool = ctx.enter_context(tc.tile_pool(name="xg", bufs=3))
+        l_pool = ctx.enter_context(tc.tile_pool(name="lp", bufs=6))
+        n_pool = ctx.enter_context(tc.tile_pool(name="np", bufs=3))
+        small = ctx.enter_context(tc.tile_pool(name="small", bufs=4))
+        rope = ctx.enter_context(tc.tile_pool(name="rope", bufs=2))
+        rkeep = ctx.enter_context(tc.tile_pool(name="rkeep", bufs=5))
+        outp = ctx.enter_context(tc.tile_pool(name="outp", bufs=3))
+        ps_xt = ctx.enter_context(tc.psum_pool(name="ps_xt", bufs=2))
+        ps_l = ctx.enter_context(tc.psum_pool(name="ps_l", bufs=2))
+        ps_r = ctx.enter_context(tc.psum_pool(name="ps_r", bufs=1))
+        ps_nt = ctx.enter_context(tc.psum_pool(name="ps_nt", bufs=1))
+        ps_kv = ctx.enter_context(tc.psum_pool(name="ps_kv", bufs=2))
+
+        wd_raw = const.tile([P, 2, 4, 640], BF16, name="wd_raw")
+        wd_src = Wkv_down.rearrange("(a q e) c -> q a (e c)", a=4, q=P, e=2)
+        wd_dst = wd_raw[:].rearrange("q g (u e) c -> q (g u) (e c)", u=2, e=2)
+        x_sb = []
+
+        def load_x(G, pieces):
+            b, g = divmod(G, 2)
+            x_sb.append(xres.tile([P, 4096], BF16, name="x_sb"))
+            src = X[b, g * 512 : (g + 1) * 512, :].rearrange("(p t) k -> p t k", t=4)
+            dst = x_sb[G][:].rearrange("p (t k) -> p t k", t=4)
+            w = 4 // pieces
+            for k in range(pieces):
+                nc.sync.dma_start(out=dst[:, k * w : (k + 1) * w, :], in_=src[:, k * w : (k + 1) * w, :])
+
+        brow = const.tile([P, 1536], BF16, name="brow")
+        nc.vector.memset(brow[:].bitcast(I32), 0)
+        nc.sync.dma_start(out=brow[0:1, 0:640], in_=bkv_down.rearrange("(o n) -> o n", o=1))
+        nc.sync.dma_start(out=brow[0:1, 640:1152], in_=bkv_up.rearrange("(o n) -> o n", o=1))
+        nc.sync.dma_start(out=wd_dst[:, 0:2, :], in_=wd_src[:, 0:2, :])
+        nc.sync.dma_start(out=wd_dst[:, 2:4, :], in_=wd_src[:, 2:4, :])
+        load_x(0, 2)
+        wu_raw = const.tile([P, 4, 512], BF16, name="wu_raw")
+        nc.sync.dma_start(out=wu_raw[:], in_=Wkv_up.rearrange("(j p) n -> p j n", j=4, p=P))
+        for G in range(1, 6):
+            load_x(G, 1)
+
+        ones = const.tile([P, P], BF16, name="ones")
+        nc.vector.memset(ones[:], 1.0)
+        eps_t = const.tile([P, 1], F32, name="eps_t")
+        nc.vector.memset(eps_t[:], EPS)
+
+        ident_f = const.tile([P, P], F32, name="ident_f")
+        make_identity(nc, ident_f[:])
+        ident_b = const.tile([P, P], BF16, name="ident_b")
+        make_identity(nc, ident_b[:])
+
+        posrep = const.tile([P, 8, 64], F32, name="posrep")
+        nc.gpsimd.iota(
+            posrep[:],
+            pattern=[[512, 2], [1, 4], [0, 64]],
+            base=0,
+            channel_multiplier=4,
+            allow_small_or_imprecise_dtypes=True,
+        )
+        tf = const.tile([P, 64], F32, name="tf")
+        nc.vector.memset(tf[:, 0:1], 1.0)
+        nc.vector.tensor_scalar_mul(out=tf[:, 0:1], in0=tf[:, 0:1], scalar1=1.0 / TWO_PI)
+        ratio = 10000.0 ** (-1.0 / 64.0)
+        n = 1
+        while n < 64:
+            nc.vector.tensor_scalar_mul(out=tf[:, n : 2 * n], in0=tf[:, 0:n], scalar1=ratio**n)
+            n *= 2
+        turns = const.tile([P, 2, 8, 64], F32, name="turns")
+        nc.vector.tensor_tensor(
+            out=turns[:, 0], in0=posrep[:], in1=tf[:].unsqueeze(1).to_broadcast([P, 8, 64]), op=ALU.mult
+        )
+        nc.vector.tensor_scalar_add(out=turns[:, 1], in0=turns[:, 0], scalar1=0.25)
+        whole = const.tile([P, 2, 8, 64], I32, name="whole")
+        nc.vector.tensor_copy(out=whole[:], in_=turns[:])
+        frac = turns
+        nc.vector.tensor_tensor(out=frac[:], in0=turns[:], in1=whole[:], op=ALU.subtract)
+        negw = turns
+        fl = "p a b c -> p (a b c)"
+        nc.vector.scalar_tensor_tensor(
+            out=negw[:].rearrange(fl),
+            in0=frac[:].rearrange(fl),
+            scalar=0.5,
+            in1=frac[:].rearrange(fl),
+            op0=ALU.is_ge,
+            op1=ALU.subtract,
+        )
+        cos2 = const.tile([P, 8, 128], F32, name="cos2")
+        sin2 = const.tile([P, 8, 128], F32, name="sin2")
+        nc.scalar.activation(out=sin2[:, :, 0:64], in_=negw[:, 0], func=AF.Sin, scale=TWO_PI)
+        nc.scalar.activation(out=sin2[:, :, 64:128], in_=negw[:, 0], func=AF.Sin, scale=-TWO_PI)
+        nc.scalar.activation(out=cos2[:, :, 0:64], in_=negw[:, 1], func=AF.Sin, scale=-TWO_PI)
+        nc.scalar.activation(out=cos2[:, :, 64:128], in_=negw[:, 1], func=AF.Sin, scale=-TWO_PI)
+
+        bias_sb = const.tile([P, 1152], F32, name="bias_sb")
+        for k in range(3):
+            bps = ps_l.tile([P, 512], F32, name="bps", tag="l_ps")
+            nc.tensor.matmul(bps[:], lhsT=ones[:], rhs=brow[:, k * 512 : (k + 1) * 512], start=True, stop=True)
+            w = min(512, 1152 - k * 512)
+            nc.scalar.copy(out=bias_sb[:, k * 512 : k * 512 + w], in_=bps[:, 0:w])
+
+        wdg = const.tile([P, 2, 640, 4], BF16, name="wdg", align_bytes=64)
+        wdc = const.tile([P, 2, 640], U32, name="wdc", align_bytes=64)
+        wds = const.tile([P, 2, 640], U8, name="wds", align_bytes=64)
+        def regroup_wd(eng_copy, g, lo, hi):
+            eng_copy(
+                out=wdg[:, g, lo:hi, :].rearrange("q (c i) j -> q c j i", i=4),
+                in_=wd_raw[:, g, :, lo:hi].rearrange("q j (c i) -> q c j i", i=4),
+            )
+
+        regroup_wd(nc.vector.tensor_copy, 0, 0, 640)
+        regroup_wd(nc.scalar.copy, 1, 0, 256)
+        regroup_wd(nc.vector.tensor_copy, 1, 256, 640)
+        for g in range(2):
+            for lo, hi in ((128, 640), (0, 128)):
+                nc.vector.quantize_mx(
+                    out=wdc[:, g, lo:hi].bitcast(FP8X4),
+                    scales=wds[:, g, lo:hi],
+                    in_=wdg[:, g, lo:hi, :].rearrange("q c j -> q (c j)"),
+                )
+        wug = const.tile([P, 512, 4], BF16, name="wug", align_bytes=64)
+        wuc = const.tile([P, 512], U32, name="wuc", align_bytes=64)
+        wus = const.tile([P, 512], U8, name="wus", align_bytes=64)
+
+        def prep_wu():
+            nc.vector.tensor_copy(
+                out=wug[:].rearrange("q (c i) j -> q c j i", i=4),
+                in_=wu_raw[:].rearrange("q j (c i) -> q c j i", i=4),
+            )
+            nc.vector.quantize_mx(
+                out=wuc[:].bitcast(FP8X4), scales=wus[:], in_=wug[:].rearrange("q c j -> q (c j)")
+            )
+
+        st = {}
+
+        def stage_a(i):
+            G, half = divmod(i, 2)
+            xw = x_sb[G][:].bitcast(F32)
+            xg = xg_pool.tile([P, 2048], BF16, name="xg", align_bytes=64)
+            xgw = xg[:].bitcast(F32)
+            for a in range(2):
+                t = 2 * half + a
+                xt = ps_xt.tile([P, 4, P], F32, name="xt")
+                for j in range(4):
+                    c0 = t * 512 + j * P
+                    nc.tensor.transpose(xt[:, j, :], xw[:, c0 : c0 + P], ident_f[:])
+                nc.scalar.copy(
+                    out=xgw[:, a * 512 : (a + 1) * 512].rearrange("q (g t u) -> q g t u", g=2, t=P, u=2),
+                    in_=xt[:].rearrange("q (g u) t -> q g t u", g=2, u=2),
+                )
+            xc = xg_pool.tile([P, 512], U32, name="xc", align_bytes=64)
+            xs = xg_pool.tile([P, 512], U8, name="xs", align_bytes=64)
+            nc.vector.quantize_mx(out=xc[:].bitcast(FP8X4), scales=xs[:], in_=xg[:])
+            st[("x", i)] = (xc, xs)
+
+        def stage_c(i):
+            G, half = divmod(i, 2)
+            xc, xs = st.pop(("x", i))
+            r_ps = ps_r.tile([P, 2, P], F32, name="r_ps")
+            l_sbs = []
+            for a in range(2):
+                l_ps = ps_l.tile([P, 512], F32, name="l_ps")
+                for g in range(2):
+                    o = a * 256 + g * P
+                    nc.tensor.matmul_mx(
+                        out=l_ps[:],
+                        lhsT=xc[:, o : o + P].bitcast(FP8X4),
+                        lhsT_scale=xs[:, o : o + P],
+                        rhs=wdc[:, g, 128:640].bitcast(FP8X4),
+                        rhs_scale=wds[:, g, 128:640],
+                        start=(g == 0),
+                        stop=(g == 1),
+                    )
+                    nc.tensor.matmul_mx(
+                        out=r_ps[:, a, :],
+                        lhsT=xc[:, o : o + P].bitcast(FP8X4),
+                        lhsT_scale=xs[:, o : o + P],
+                        rhs=wdc[:, g, 0:128].bitcast(FP8X4),
+                        rhs_scale=wds[:, g, 0:128],
+                        start=(g == 0),
+                        stop=(g == 1),
+                    )
+                l_sb = l_pool.tile([P, 512], F32, name="l_sb")
+                nc.vector.tensor_tensor(out=l_sb[:], in0=l_ps[:], in1=bias_sb[:, 128:640], op=ALU.add)
+                l_sbs.append(l_sb)
+            r_sb = rkeep.tile([P, 2, P], F32, name="r_sb")
+            nc.vector.tensor_tensor(
+                out=r_sb[:],
+                in0=r_ps[:],
+                in1=bias_sb[:, 0:128].unsqueeze(1).to_broadcast([P, 2, P]),
+                op=ALU.add,
+            )
+            ss = small.tile([P, 2], F32, name="ss")
+            for a in range(2):
+                junk = small.tile([P, 512], BF16, name="junk")
+                nc.scalar.activation(out=junk[:], in_=l_sbs[a][:], func=AF.Square, accum_out=ss[:, a : a + 1])
+            rms = small.tile([P, 2], F32, name="rms")
+            nc.scalar.activation(out=rms[:], in_=ss[:], func=AF.Sqrt, scale=1.0 / 512.0, bias=eps_t[:, 0:1])
+            rstd = small.tile([P, 2], F32, name="rstd")
+            nc.vector.reciprocal(out=rstd[:], in_=rms[:])
+            n_bf = n_pool.tile([P, 2, 512], BF16, name="n_bf")
+            for a in range(2):
+                nc.vector.tensor_scalar_mul(out=n_bf[:, a, :], in0=l_sbs[a][:], scalar1=rstd[:, a : a + 1])
+            st[("n", i)] = n_bf
+            st[("r", i)] = r_sb
+
+        def stage_r(i):
+            G, half = divmod(i, 2)
+            r_sb = st.pop(("r", i))
+            if half == 0:
+                key_sb = outp.tile([P, 4, 4, 192], F32, name="key_sb")
+                val_sb = outp.tile([P, 4, 4, 64], F32, name="val_sb")
+                st[("o", G)] = (key_sb, val_sb)
+            key_sb, val_sb = st[("o", G)]
+            t0 = 2 * half
+            gt = (G % 2) * 4 + t0
+            m1 = rope.tile([P, 2, P], F32, name="m1")
+            m2 = rope.tile([P, 2, P], F32, name="m2")
+            nc.gpsimd.tensor_tensor(out=m1[:], in0=r_sb[:], in1=cos2[:, gt : gt + 2, :], op=ALU.mult)
+            nc.gpsimd.tensor_tensor(
+                out=m2[:, :, 0:64], in0=r_sb[:, :, 64:128], in1=sin2[:, gt : gt + 2, 0:64], op=ALU.mult
+            )
+            nc.gpsimd.tensor_tensor(
+                out=m2[:, :, 64:128], in0=r_sb[:, :, 0:64], in1=sin2[:, gt : gt + 2, 64:128], op=ALU.mult
+            )
+            nc.gpsimd.tensor_tensor(
+                out=key_sb[:, :, t0 : t0 + 2, 64:192],
+                in0=m1[:].unsqueeze(1).to_broadcast([P, 4, 2, P]),
+                in1=m2[:].unsqueeze(1).to_broadcast([P, 4, 2, P]),
+                op=ALU.add,
+            )
+
+        def stage_e(i):
+            n_bf = st.pop(("n", i))
+            nt = ps_nt.tile([P, 2, 4, P], BF16, name="nt")
+            for a in range(2):
+                for j in range(4):
+                    nc.tensor.transpose(nt[:, a, j, :], n_bf[:, a, j * P : (j + 1) * P], ident_b[:])
+            ng = n_pool.tile([P, 1024], BF16, name="ng", align_bytes=64)
+            nc.scalar.copy(
+                out=ng[:].rearrange("p (a t j) -> p a t j", a=2, t=P, j=4),
+                in_=nt[:].rearrange("p a j t -> p a t j"),
+            )
+            ncd = n_pool.tile([P, 256], U32, name="ncd", align_bytes=64)
+            nsc = n_pool.tile([P, 256], U8, name="nsc", align_bytes=64)
+            nc.vector.quantize_mx(out=ncd[:].bitcast(FP8X4), scales=nsc[:], in_=ng[:])
+            st[("q", i)] = (ncd, nsc)
+
+        def stage_g(i):
+            G, half = divmod(i, 2)
+            ncd, nsc = st.pop(("q", i))
+            key_sb, val_sb = st[("o", G)]
+            buv = bias_sb[:, 640:1152].rearrange("p (h x d) -> p h x d", h=4, x=2, d=64)
+            for a in range(2):
+                t = 2 * half + a
+                kv = ps_kv.tile([P, 512], F32, name="kv")
+                nc.tensor.matmul_mx(
+                    out=kv[:],
+                    lhsT=ncd[:, a * P : (a + 1) * P].bitcast(FP8X4),
+                    lhsT_scale=nsc[:, a * P : (a + 1) * P],
+                    rhs=wuc[:].bitcast(FP8X4),
+                    rhs_scale=wus[:],
+                    start=True,
+                    stop=True,
+                )
+                kvv = kv[:].rearrange("p (h x d) -> p h x d", h=4, x=2, d=64)
+                nc.vector.tensor_tensor(out=key_sb[:, :, t, 0:64], in0=kvv[:, :, 0, :], in1=buv[:, :, 0, :], op=ALU.add)
+                nc.vector.tensor_tensor(out=val_sb[:, :, t, :], in0=kvv[:, :, 1, :], in1=buv[:, :, 1, :], op=ALU.add)
+            b, g = divmod(G, 2)
+            if G == NQUAD - 1:
+                lo, hi = 2 * half, 2 * half + 2
+            else:
+                lo, hi = 0, 4
+            if half == 1 or G == NQUAD - 1:
+                nc.sync.dma_start(
+                    out=out_0[b].rearrange("h (g p t) d -> g p h t d", g=2, p=P, t=4)[g][:, :, lo:hi, :],
+                    in_=key_sb[:, :, lo:hi, :],
+                )
+                nc.sync.dma_start(
+                    out=out_1[b].rearrange("h (g p t) d -> g p h t d", g=2, p=P, t=4)[g][:, :, lo:hi, :],
+                    in_=val_sb[:, :, lo:hi, :],
+                )
+            if half == 1:
+                st.pop(("o", G))
+
+        if PIN:
+            ctx.enter_context(tc.manual_schedule())
+        for i in range(NPAIR + 4):
+            if i < NPAIR:
+                stage_a(i)
+                if i % 2 == 1 and i // 2 + 6 < NQUAD:
+                    load_x(i // 2 + 6, 1)
+            if 0 <= i - 3 < NPAIR:
+                stage_e(i - 3)
+                stage_r(i - 3)
+            if i == 2:
+                prep_wu()
+            if 0 <= i - 1 < NPAIR:
+                stage_c(i - 1)
+            if 0 <= i - 4 < NPAIR:
+                stage_g(i - 4)

@@ -20,14 +20,13 @@ NQUAD = 8
 NPAIR = 16
 EPS = 1e-6
 TWO_PI = 2.0 * math.pi
-PIN = False
 
 
 def tile_mla_pb_t_kernel(tc, X, Wkv_down, bkv_down, Wkv_up, bkv_up, out_0, out_1):
     nc = tc.nc
     with ExitStack() as ctx:
         const = ctx.enter_context(tc.tile_pool(name="const", bufs=1))
-        xres = ctx.enter_context(tc.tile_pool(name="xres", bufs=6))
+        xres = ctx.enter_context(tc.tile_pool(name="xres", bufs=NQUAD))
         xg_pool = ctx.enter_context(tc.tile_pool(name="xg", bufs=3))
         l_pool = ctx.enter_context(tc.tile_pool(name="lp", bufs=6))
         n_pool = ctx.enter_context(tc.tile_pool(name="np", bufs=3))
@@ -57,30 +56,32 @@ def tile_mla_pb_t_kernel(tc, X, Wkv_down, bkv_down, Wkv_up, bkv_up, out_0, out_1
 
         brow = const.tile([P, 1536], BF16, name="brow")
         nc.vector.memset(brow[:].bitcast(I32), 0)
+        nc.sync.dma_start(out=wd_dst[:, 0:2, :], in_=wd_src[:, 0:2, :])
         nc.sync.dma_start(out=brow[0:1, 0:640], in_=bkv_down.rearrange("(o n) -> o n", o=1))
         nc.sync.dma_start(out=brow[0:1, 640:1152], in_=bkv_up.rearrange("(o n) -> o n", o=1))
-        nc.sync.dma_start(out=wd_dst[:, 0:2, :], in_=wd_src[:, 0:2, :])
         nc.sync.dma_start(out=wd_dst[:, 2:4, :], in_=wd_src[:, 2:4, :])
         load_x(0, 2)
         wu_raw = const.tile([P, 4, 512], BF16, name="wu_raw")
-        nc.sync.dma_start(out=wu_raw[:], in_=Wkv_up.rearrange("(j p) n -> p j n", j=4, p=P))
-        for G in range(1, 6):
+        nc.sync.dma_start(
+            out=wu_raw[:].rearrange("p (u e) n -> p u (e n)", u=2),
+            in_=Wkv_up.rearrange("(u p e) n -> p u (e n)", u=2, p=P, e=2),
+        )
+        for G in range(1, NQUAD):
             load_x(G, 1)
 
         ones = const.tile([P, P], BF16, name="ones")
         nc.vector.memset(ones[:], 1.0)
         eps_t = const.tile([P, 1], F32, name="eps_t")
-        nc.vector.memset(eps_t[:], EPS)
+        nc.vector.memset(eps_t[:], 0.0)
+        nc.vector.tensor_scalar_add(out=eps_t[:], in0=eps_t[:], scalar1=EPS)
 
         ident_f = const.tile([P, P], F32, name="ident_f")
         make_identity(nc, ident_f[:])
-        ident_b = const.tile([P, P], BF16, name="ident_b")
-        make_identity(nc, ident_b[:])
 
-        posrep = const.tile([P, 8, 64], F32, name="posrep")
+        pos = const.tile([P, 8], F32, name="pos")
         nc.gpsimd.iota(
-            posrep[:],
-            pattern=[[512, 2], [1, 4], [0, 64]],
+            pos[:],
+            pattern=[[512, 2], [1, 4]],
             base=0,
             channel_multiplier=4,
             allow_small_or_imprecise_dtypes=True,
@@ -95,12 +96,15 @@ def tile_mla_pb_t_kernel(tc, X, Wkv_down, bkv_down, Wkv_up, bkv_up, out_0, out_1
             n *= 2
         turns = const.tile([P, 2, 8, 64], F32, name="turns")
         nc.vector.tensor_tensor(
-            out=turns[:, 0], in0=posrep[:], in1=tf[:].unsqueeze(1).to_broadcast([P, 8, 64]), op=ALU.mult
+            out=turns[:, 0],
+            in0=pos[:].unsqueeze(2).to_broadcast([P, 8, 64]),
+            in1=tf[:].unsqueeze(1).to_broadcast([P, 8, 64]),
+            op=ALU.mult,
         )
         nc.vector.tensor_scalar_add(out=turns[:, 1], in0=turns[:, 0], scalar1=0.25)
         whole = const.tile([P, 2, 8, 64], I32, name="whole")
         nc.vector.tensor_copy(out=whole[:], in_=turns[:])
-        frac = turns
+        frac = const.tile([P, 2, 8, 64], F32, name="frac")
         nc.vector.tensor_tensor(out=frac[:], in0=turns[:], in1=whole[:], op=ALU.subtract)
         negw = turns
         fl = "p a b c -> p (a b c)"
@@ -112,12 +116,13 @@ def tile_mla_pb_t_kernel(tc, X, Wkv_down, bkv_down, Wkv_up, bkv_up, out_0, out_1
             op0=ALU.is_ge,
             op1=ALU.subtract,
         )
-        cos2 = const.tile([P, 8, 128], F32, name="cos2")
-        sin2 = const.tile([P, 8, 128], F32, name="sin2")
-        nc.scalar.activation(out=sin2[:, :, 0:64], in_=negw[:, 0], func=AF.Sin, scale=TWO_PI)
-        nc.scalar.activation(out=sin2[:, :, 64:128], in_=negw[:, 0], func=AF.Sin, scale=-TWO_PI)
-        nc.scalar.activation(out=cos2[:, :, 0:64], in_=negw[:, 1], func=AF.Sin, scale=-TWO_PI)
-        nc.scalar.activation(out=cos2[:, :, 64:128], in_=negw[:, 1], func=AF.Sin, scale=-TWO_PI)
+        cos_t = const.tile([P, 8, 64], F32, name="cos_t")
+        sin_t = const.tile([P, 8, 2, 64], F32, name="sin_t")
+        nc.scalar.activation(out=sin_t[:, :, 0, :], in_=negw[:, 0], func=AF.Sin, scale=TWO_PI)
+        nc.scalar.activation(out=cos_t[:], in_=negw[:, 1], func=AF.Sin, scale=-TWO_PI)
+        nc.gpsimd.tensor_scalar(
+            out=sin_t[:, :, 1, :], in0=sin_t[:, :, 0, :], scalar1=-1.0, scalar2=0.0, op0=ALU.mult, op1=ALU.add
+        )
 
         bias_sb = const.tile([P, 1152], F32, name="bias_sb")
         for k in range(3):
@@ -129,6 +134,7 @@ def tile_mla_pb_t_kernel(tc, X, Wkv_down, bkv_down, Wkv_up, bkv_up, out_0, out_1
         wdg = const.tile([P, 2, 640, 4], BF16, name="wdg", align_bytes=64)
         wdc = const.tile([P, 2, 640], U32, name="wdc", align_bytes=64)
         wds = const.tile([P, 2, 640], U8, name="wds", align_bytes=64)
+
         def regroup_wd(eng_copy, g, lo, hi):
             eng_copy(
                 out=wdg[:, g, lo:hi, :].rearrange("q (c i) j -> q c j i", i=4),
@@ -181,7 +187,6 @@ def tile_mla_pb_t_kernel(tc, X, Wkv_down, bkv_down, Wkv_up, bkv_up, out_0, out_1
             st[("x", i)] = (xc, xs)
 
         def stage_c(i):
-            G, half = divmod(i, 2)
             xc, xs = st.pop(("x", i))
             r_ps = ps_r.tile([P, 2, P], F32, name="r_ps")
             l_sbs = []
@@ -227,7 +232,10 @@ def tile_mla_pb_t_kernel(tc, X, Wkv_down, bkv_down, Wkv_up, bkv_up, out_0, out_1
             nc.vector.reciprocal(out=rstd[:], in_=rms[:])
             n_bf = n_pool.tile([P, 2, 512], BF16, name="n_bf")
             for a in range(2):
-                nc.vector.tensor_scalar_mul(out=n_bf[:, a, :], in0=l_sbs[a][:], scalar1=rstd[:, a : a + 1])
+                if a == 1 and i % 2 == 1:
+                    nc.vector.tensor_scalar_mul(out=n_bf[:, a, :], in0=l_sbs[a][:], scalar1=rstd[:, a : a + 1])
+                else:
+                    nc.scalar.activation(out=n_bf[:, a, :], in_=l_sbs[a][:], func=AF.Copy, scale=rstd[:, a : a + 1])
             st[("n", i)] = n_bf
             st[("r", i)] = r_sb
 
@@ -241,32 +249,46 @@ def tile_mla_pb_t_kernel(tc, X, Wkv_down, bkv_down, Wkv_up, bkv_up, out_0, out_1
             key_sb, val_sb = st[("o", G)]
             t0 = 2 * half
             gt = (G % 2) * 4 + t0
-            m1 = rope.tile([P, 2, P], F32, name="m1")
-            m2 = rope.tile([P, 2, P], F32, name="m2")
-            nc.gpsimd.tensor_tensor(out=m1[:], in0=r_sb[:], in1=cos2[:, gt : gt + 2, :], op=ALU.mult)
+            rv = r_sb[:].rearrange("p a (h d) -> p a h d", h=2)
+            m1 = rope.tile([P, 2, 2, 64], F32, name="m1")
+            m2 = rope.tile([P, 2, 2, 64], F32, name="m2")
             nc.gpsimd.tensor_tensor(
-                out=m2[:, :, 0:64], in0=r_sb[:, :, 64:128], in1=sin2[:, gt : gt + 2, 0:64], op=ALU.mult
+                out=m1[:],
+                in0=rv,
+                in1=cos_t[:, gt : gt + 2, :].unsqueeze(2).to_broadcast([P, 2, 2, 64]),
+                op=ALU.mult,
             )
             nc.gpsimd.tensor_tensor(
-                out=m2[:, :, 64:128], in0=r_sb[:, :, 0:64], in1=sin2[:, gt : gt + 2, 64:128], op=ALU.mult
+                out=m2[:], in0=rv[:, :, ::-1, :], in1=sin_t[:, gt : gt + 2, :, :], op=ALU.mult
             )
+            first = key_sb[:, 0, t0 : t0 + 2, 64:192]
             nc.gpsimd.tensor_tensor(
-                out=key_sb[:, :, t0 : t0 + 2, 64:192],
-                in0=m1[:].unsqueeze(1).to_broadcast([P, 4, 2, P]),
-                in1=m2[:].unsqueeze(1).to_broadcast([P, 4, 2, P]),
+                out=first,
+                in0=m1[:].rearrange("p a h d -> p a (h d)"),
+                in1=m2[:].rearrange("p a h d -> p a (h d)"),
                 op=ALU.add,
+            )
+            nc.gpsimd.tensor_scalar(
+                out=key_sb[:, 1:4, t0 : t0 + 2, 64:192],
+                in0=first.unsqueeze(1).to_broadcast([P, 3, 2, P]),
+                scalar1=1.0,
+                scalar2=0.0,
+                op0=ALU.mult,
+                op1=ALU.add,
             )
 
         def stage_e(i):
             n_bf = st.pop(("n", i))
-            nt = ps_nt.tile([P, 2, 4, P], BF16, name="nt")
+            nw = n_bf[:].rearrange("p a c -> p (a c)").bitcast(F32)
+            nt = ps_nt.tile([P, 2, 2, P], F32, name="nt")
             for a in range(2):
-                for j in range(4):
-                    nc.tensor.transpose(nt[:, a, j, :], n_bf[:, a, j * P : (j + 1) * P], ident_b[:])
+                for u in range(2):
+                    c0 = a * 256 + u * P
+                    nc.tensor.transpose(nt[:, a, u, :], nw[:, c0 : c0 + P], ident_f[:])
             ng = n_pool.tile([P, 1024], BF16, name="ng", align_bytes=64)
             nc.scalar.copy(
-                out=ng[:].rearrange("p (a t j) -> p a t j", a=2, t=P, j=4),
-                in_=nt[:].rearrange("p a j t -> p a t j"),
+                out=ng[:].bitcast(F32).rearrange("p (a t u) -> p a t u", a=2, t=P, u=2),
+                in_=nt[:].rearrange("p a u t -> p a t u"),
             )
             ncd = n_pool.tile([P, 256], U32, name="ncd", align_bytes=64)
             nsc = n_pool.tile([P, 256], U8, name="nsc", align_bytes=64)
@@ -310,13 +332,9 @@ def tile_mla_pb_t_kernel(tc, X, Wkv_down, bkv_down, Wkv_up, bkv_up, out_0, out_1
             if half == 1:
                 st.pop(("o", G))
 
-        if PIN:
-            ctx.enter_context(tc.manual_schedule())
         for i in range(NPAIR + 4):
             if i < NPAIR:
                 stage_a(i)
-                if i % 2 == 1 and i // 2 + 6 < NQUAD:
-                    load_x(i // 2 + 6, 1)
             if 0 <= i - 3 < NPAIR:
                 stage_e(i - 3)
                 stage_r(i - 3)

@@ -32,7 +32,7 @@ def tile_mla_pb_t_kernel(tc, X, Wkv_down, bkv_down, Wkv_up, bkv_up, out_0, out_1
         n_pool = ctx.enter_context(tc.tile_pool(name="np", bufs=3))
         small = ctx.enter_context(tc.tile_pool(name="small", bufs=4))
         rope = ctx.enter_context(tc.tile_pool(name="rope", bufs=2))
-        rkeep = ctx.enter_context(tc.tile_pool(name="rkeep", bufs=5))
+        rkeep = ctx.enter_context(tc.tile_pool(name="rkeep", bufs=4))
         outp = ctx.enter_context(tc.tile_pool(name="outp", bufs=3))
         ps_xt = ctx.enter_context(tc.psum_pool(name="ps_xt", bufs=2))
         ps_l = ctx.enter_context(tc.psum_pool(name="ps_l", bufs=2))
@@ -40,9 +40,12 @@ def tile_mla_pb_t_kernel(tc, X, Wkv_down, bkv_down, Wkv_up, bkv_up, out_0, out_1
         ps_nt = ctx.enter_context(tc.psum_pool(name="ps_nt", bufs=1))
         ps_kv = ctx.enter_context(tc.psum_pool(name="ps_kv", bufs=2))
 
+        ctx.enter_context(tc.manual_schedule())
+
         wd_raw = const.tile([P, 2, 4, 640], BF16, name="wd_raw")
         wd_src = Wkv_down.rearrange("(a q e) c -> q a (e c)", a=4, q=P, e=2)
         wd_dst = wd_raw[:].rearrange("q g (u e) c -> q (g u) (e c)", u=2, e=2)
+        wu_raw = const.tile([P, 4, 512], BF16, name="wu_raw")
         x_sb = []
 
         def load_x(G, pieces):
@@ -54,14 +57,13 @@ def tile_mla_pb_t_kernel(tc, X, Wkv_down, bkv_down, Wkv_up, bkv_up, out_0, out_1
             for k in range(pieces):
                 nc.sync.dma_start(out=dst[:, k * w : (k + 1) * w, :], in_=src[:, k * w : (k + 1) * w, :])
 
-        brow = const.tile([P, 1536], BF16, name="brow")
+        brow = const.tile([P, 1152], BF16, name="brow")
         nc.vector.memset(brow[:].bitcast(I32), 0)
         nc.sync.dma_start(out=wd_dst[:, 0:2, :], in_=wd_src[:, 0:2, :])
         nc.sync.dma_start(out=brow[0:1, 0:640], in_=bkv_down.rearrange("(o n) -> o n", o=1))
         nc.sync.dma_start(out=brow[0:1, 640:1152], in_=bkv_up.rearrange("(o n) -> o n", o=1))
         nc.sync.dma_start(out=wd_dst[:, 2:4, :], in_=wd_src[:, 2:4, :])
-        load_x(0, 2)
-        wu_raw = const.tile([P, 4, 512], BF16, name="wu_raw")
+        load_x(0, 4)
         nc.sync.dma_start(
             out=wu_raw[:].rearrange("p (u e) n -> p u (e n)", u=2),
             in_=Wkv_up.rearrange("(u p e) n -> p u (e n)", u=2, p=P, e=2),
@@ -87,49 +89,45 @@ def tile_mla_pb_t_kernel(tc, X, Wkv_down, bkv_down, Wkv_up, bkv_up, out_0, out_1
             allow_small_or_imprecise_dtypes=True,
         )
         tf = const.tile([P, 64], F32, name="tf")
-        nc.vector.memset(tf[:, 0:1], 1.0)
-        nc.vector.tensor_scalar_mul(out=tf[:, 0:1], in0=tf[:, 0:1], scalar1=1.0 / TWO_PI)
+        nc.gpsimd.memset(tf[:, 0:1], 1.0)
+
+        def g_scale(out, in_, factor, offset=0.0):
+            nc.gpsimd.tensor_scalar(out=out, in0=in_, scalar1=factor, scalar2=offset, op0=ALU.mult, op1=ALU.add)
+
+        g_scale(tf[:, 0:1], tf[:, 0:1], 1.0 / TWO_PI)
         ratio = 10000.0 ** (-1.0 / 64.0)
         n = 1
         while n < 64:
-            nc.vector.tensor_scalar_mul(out=tf[:, n : 2 * n], in0=tf[:, 0:n], scalar1=ratio**n)
+            g_scale(tf[:, n : 2 * n], tf[:, 0:n], ratio**n)
             n *= 2
         turns = const.tile([P, 2, 8, 64], F32, name="turns")
-        nc.vector.tensor_tensor(
+        nc.gpsimd.tensor_tensor(
             out=turns[:, 0],
             in0=pos[:].unsqueeze(2).to_broadcast([P, 8, 64]),
             in1=tf[:].unsqueeze(1).to_broadcast([P, 8, 64]),
             op=ALU.mult,
         )
-        nc.vector.tensor_scalar_add(out=turns[:, 1], in0=turns[:, 0], scalar1=0.25)
+        g_scale(turns[:, 1], turns[:, 0], 1.0, 0.25)
         whole = const.tile([P, 2, 8, 64], I32, name="whole")
-        nc.vector.tensor_copy(out=whole[:], in_=turns[:])
         frac = const.tile([P, 2, 8, 64], F32, name="frac")
-        nc.vector.tensor_tensor(out=frac[:], in0=turns[:], in1=whole[:], op=ALU.subtract)
-        negw = turns
-        fl = "p a b c -> p (a b c)"
-        nc.vector.scalar_tensor_tensor(
-            out=negw[:].rearrange(fl),
-            in0=frac[:].rearrange(fl),
-            scalar=0.5,
-            in1=frac[:].rearrange(fl),
-            op0=ALU.is_ge,
-            op1=ALU.subtract,
-        )
         cos_t = const.tile([P, 8, 64], F32, name="cos_t")
         sin_t = const.tile([P, 8, 2, 64], F32, name="sin_t")
-        nc.scalar.activation(out=sin_t[:, :, 0, :], in_=negw[:, 0], func=AF.Sin, scale=TWO_PI)
-        nc.scalar.activation(out=cos_t[:], in_=negw[:, 1], func=AF.Sin, scale=-TWO_PI)
-        nc.gpsimd.tensor_scalar(
-            out=sin_t[:, :, 1, :], in0=sin_t[:, :, 0, :], scalar1=-1.0, scalar2=0.0, op0=ALU.mult, op1=ALU.add
-        )
+
+        def wrap_turns():
+            nc.vector.tensor_copy(out=whole[:], in_=turns[:])
+            nc.vector.tensor_tensor(out=frac[:], in0=turns[:], in1=whole[:], op=ALU.subtract)
+
+        def make_tables():
+            nc.scalar.activation(out=sin_t[:, :, 1, :], in_=frac[:, 0], func=AF.Sin, scale=TWO_PI)
+            nc.scalar.activation(out=cos_t[:], in_=frac[:, 1], func=AF.Sin, scale=TWO_PI)
+            g_scale(sin_t[:, :, 0, :], sin_t[:, :, 1, :], -1.0)
 
         bias_sb = const.tile([P, 1152], F32, name="bias_sb")
-        for k in range(3):
-            bps = ps_l.tile([P, 512], F32, name="bps", tag="l_ps")
-            nc.tensor.matmul(bps[:], lhsT=ones[:], rhs=brow[:, k * 512 : (k + 1) * 512], start=True, stop=True)
-            w = min(512, 1152 - k * 512)
-            nc.scalar.copy(out=bias_sb[:, k * 512 : k * 512 + w], in_=bps[:, 0:w])
+
+        def spread_bias(eng_copy, pool, tag, lo, hi):
+            bps = pool.tile([P, 512], F32, name="bps", tag=tag)
+            nc.tensor.matmul(bps[:, 0 : hi - lo], lhsT=ones[:], rhs=brow[:, lo:hi], start=True, stop=True)
+            eng_copy(out=bias_sb[:, lo:hi], in_=bps[:, 0 : hi - lo])
 
         wdg = const.tile([P, 2, 640, 4], BF16, name="wdg", align_bytes=64)
         wdc = const.tile([P, 2, 640], U32, name="wdc", align_bytes=64)
@@ -141,16 +139,23 @@ def tile_mla_pb_t_kernel(tc, X, Wkv_down, bkv_down, Wkv_up, bkv_up, out_0, out_1
                 in_=wd_raw[:, g, :, lo:hi].rearrange("q j (c i) -> q c j i", i=4),
             )
 
-        regroup_wd(nc.vector.tensor_copy, 0, 0, 640)
-        regroup_wd(nc.scalar.copy, 1, 0, 256)
-        regroup_wd(nc.vector.tensor_copy, 1, 256, 640)
+        def quantise_wd(g, lo, hi):
+            nc.vector.quantize_mx(
+                out=wdc[:, g, lo:hi].bitcast(FP8X4),
+                scales=wds[:, g, lo:hi],
+                in_=wdg[:, g, lo:hi, :].rearrange("q c j -> q (c j)"),
+            )
+
         for g in range(2):
-            for lo, hi in ((128, 640), (0, 128)):
-                nc.vector.quantize_mx(
-                    out=wdc[:, g, lo:hi].bitcast(FP8X4),
-                    scales=wds[:, g, lo:hi],
-                    in_=wdg[:, g, lo:hi, :].rearrange("q c j -> q (c j)"),
-                )
+            regroup_wd(nc.vector.tensor_copy, g, 128, 512)
+            regroup_wd(nc.scalar.copy, g, 512, 640)
+            regroup_wd(nc.scalar.copy, g, 0, 128)
+            if g == 0:
+                spread_bias(nc.vector.tensor_copy, ps_l, "l_ps", 128, 640)
+                spread_bias(nc.scalar.copy, ps_l, "l_ps", 0, 128)
+        for g in range(2):
+            quantise_wd(g, 128, 640)
+            quantise_wd(g, 0, 128)
         wug = const.tile([P, 512, 4], BF16, name="wug", align_bytes=64)
         wuc = const.tile([P, 512], U32, name="wuc", align_bytes=64)
         wus = const.tile([P, 512], U8, name="wus", align_bytes=64)
@@ -166,17 +171,23 @@ def tile_mla_pb_t_kernel(tc, X, Wkv_down, bkv_down, Wkv_up, bkv_up, out_0, out_1
 
         st = {}
 
-        def stage_a(i):
+        def turn_x(i):
             G, half = divmod(i, 2)
             xw = x_sb[G][:].bitcast(F32)
-            xg = xg_pool.tile([P, 2048], BF16, name="xg", align_bytes=64)
-            xgw = xg[:].bitcast(F32)
+            xts = []
             for a in range(2):
                 t = 2 * half + a
                 xt = ps_xt.tile([P, 4, P], F32, name="xt")
                 for j in range(4):
                     c0 = t * 512 + j * P
                     nc.tensor.transpose(xt[:, j, :], xw[:, c0 : c0 + P], ident_f[:])
+                xts.append(xt)
+            st[("xt", i)] = xts
+
+        def quantise_x(i):
+            xg = xg_pool.tile([P, 2048], BF16, name="xg", align_bytes=64)
+            xgw = xg[:].bitcast(F32)
+            for a, xt in enumerate(st.pop(("xt", i))):
                 nc.scalar.copy(
                     out=xgw[:, a * 512 : (a + 1) * 512].rearrange("q (g t u) -> q g t u", g=2, t=P, u=2),
                     in_=xt[:].rearrange("q (g u) t -> q g t u", g=2, u=2),
@@ -186,32 +197,31 @@ def tile_mla_pb_t_kernel(tc, X, Wkv_down, bkv_down, Wkv_up, bkv_up, out_0, out_1
             nc.vector.quantize_mx(out=xc[:].bitcast(FP8X4), scales=xs[:], in_=xg[:])
             st[("x", i)] = (xc, xs)
 
-        def stage_c(i):
+        def down(i):
             xc, xs = st.pop(("x", i))
             r_ps = ps_r.tile([P, 2, P], F32, name="r_ps")
-            l_sbs = []
+            l_pss = []
             for a in range(2):
                 l_ps = ps_l.tile([P, 512], F32, name="l_ps")
                 for g in range(2):
                     o = a * 256 + g * P
-                    nc.tensor.matmul_mx(
-                        out=l_ps[:],
-                        lhsT=xc[:, o : o + P].bitcast(FP8X4),
-                        lhsT_scale=xs[:, o : o + P],
-                        rhs=wdc[:, g, 128:640].bitcast(FP8X4),
-                        rhs_scale=wds[:, g, 128:640],
-                        start=(g == 0),
-                        stop=(g == 1),
-                    )
-                    nc.tensor.matmul_mx(
-                        out=r_ps[:, a, :],
-                        lhsT=xc[:, o : o + P].bitcast(FP8X4),
-                        lhsT_scale=xs[:, o : o + P],
-                        rhs=wdc[:, g, 0:128].bitcast(FP8X4),
-                        rhs_scale=wds[:, g, 0:128],
-                        start=(g == 0),
-                        stop=(g == 1),
-                    )
+                    for out, lo, hi in ((l_ps[:], 128, 640), (r_ps[:, a, :], 0, 128)):
+                        nc.tensor.matmul_mx(
+                            out=out,
+                            lhsT=xc[:, o : o + P].bitcast(FP8X4),
+                            lhsT_scale=xs[:, o : o + P],
+                            rhs=wdc[:, g, lo:hi].bitcast(FP8X4),
+                            rhs_scale=wds[:, g, lo:hi],
+                            start=(g == 0),
+                            stop=(g == 1),
+                        )
+                l_pss.append(l_ps)
+            st[("d", i)] = (l_pss, r_ps)
+
+        def add_bias(i):
+            l_pss, r_ps = st.pop(("d", i))
+            l_sbs = []
+            for l_ps in l_pss:
                 l_sb = l_pool.tile([P, 512], F32, name="l_sb")
                 nc.vector.tensor_tensor(out=l_sb[:], in0=l_ps[:], in1=bias_sb[:, 128:640], op=ALU.add)
                 l_sbs.append(l_sb)
@@ -222,24 +232,34 @@ def tile_mla_pb_t_kernel(tc, X, Wkv_down, bkv_down, Wkv_up, bkv_up, out_0, out_1
                 in1=bias_sb[:, 0:128].unsqueeze(1).to_broadcast([P, 2, P]),
                 op=ALU.add,
             )
+            st[("l", i)] = l_sbs
+            st[("r", i)] = r_sb
+
+        def norm(i):
             ss = small.tile([P, 2], F32, name="ss")
             for a in range(2):
                 junk = small.tile([P, 512], BF16, name="junk")
-                nc.scalar.activation(out=junk[:], in_=l_sbs[a][:], func=AF.Square, accum_out=ss[:, a : a + 1])
-            rms = small.tile([P, 2], F32, name="rms")
-            nc.scalar.activation(out=rms[:], in_=ss[:], func=AF.Sqrt, scale=1.0 / 512.0, bias=eps_t[:, 0:1])
+                nc.scalar.activation(
+                    out=junk[:], in_=st[("l", i)][a][:], func=AF.Square, accum_out=ss[:, a : a + 1]
+                )
             rstd = small.tile([P, 2], F32, name="rstd")
-            nc.vector.reciprocal(out=rstd[:], in_=rms[:])
-            n_bf = n_pool.tile([P, 2, 512], BF16, name="n_bf")
-            for a in range(2):
-                if a == 1 and i % 2 == 1:
-                    nc.vector.tensor_scalar_mul(out=n_bf[:, a, :], in0=l_sbs[a][:], scalar1=rstd[:, a : a + 1])
-                else:
-                    nc.scalar.activation(out=n_bf[:, a, :], in_=l_sbs[a][:], func=AF.Copy, scale=rstd[:, a : a + 1])
-            st[("n", i)] = n_bf
-            st[("r", i)] = r_sb
+            nc.scalar.activation(
+                out=rstd[:], in_=ss[:], func=AF.Abs_reciprocal_sqrt, scale=1.0 / 512.0, bias=eps_t[:, 0:1]
+            )
+            st[("s", i)] = rstd
 
-        def stage_r(i):
+        def scale_n(i, a):
+            if a == 0:
+                st[("n", i)] = n_pool.tile([P, 2, 512], BF16, name="n_bf")
+            n_bf = st[("n", i)]
+            l_sb = st[("l", i)][a]
+            rstd = st[("s", i)]
+            if a == 0 or i % 3 == 0:
+                nc.scalar.activation(out=n_bf[:, a, :], in_=l_sb[:], func=AF.Copy, scale=rstd[:, a : a + 1])
+            else:
+                nc.vector.tensor_scalar_mul(out=n_bf[:, a, :], in0=l_sb[:], scalar1=rstd[:, a : a + 1])
+
+        def rotate(i):
             G, half = divmod(i, 2)
             r_sb = st.pop(("r", i))
             if half == 0:
@@ -268,16 +288,9 @@ def tile_mla_pb_t_kernel(tc, X, Wkv_down, bkv_down, Wkv_up, bkv_up, out_0, out_1
                 in1=m2[:].rearrange("p a h d -> p a (h d)"),
                 op=ALU.add,
             )
-            nc.gpsimd.tensor_scalar(
-                out=key_sb[:, 1:4, t0 : t0 + 2, 64:192],
-                in0=first.unsqueeze(1).to_broadcast([P, 3, 2, P]),
-                scalar1=1.0,
-                scalar2=0.0,
-                op0=ALU.mult,
-                op1=ALU.add,
-            )
+            g_scale(key_sb[:, 1:4, t0 : t0 + 2, 64:192], first.unsqueeze(1).to_broadcast([P, 3, 2, P]), 1.0)
 
-        def stage_e(i):
+        def turn_n(i):
             n_bf = st.pop(("n", i))
             nw = n_bf[:].rearrange("p a c -> p (a c)").bitcast(F32)
             nt = ps_nt.tile([P, 2, 2, P], F32, name="nt")
@@ -295,13 +308,10 @@ def tile_mla_pb_t_kernel(tc, X, Wkv_down, bkv_down, Wkv_up, bkv_up, out_0, out_1
             nc.vector.quantize_mx(out=ncd[:].bitcast(FP8X4), scales=nsc[:], in_=ng[:])
             st[("q", i)] = (ncd, nsc)
 
-        def stage_g(i):
-            G, half = divmod(i, 2)
+        def up(i):
             ncd, nsc = st.pop(("q", i))
-            key_sb, val_sb = st[("o", G)]
-            buv = bias_sb[:, 640:1152].rearrange("p (h x d) -> p h x d", h=4, x=2, d=64)
+            kvs = []
             for a in range(2):
-                t = 2 * half + a
                 kv = ps_kv.tile([P, 512], F32, name="kv")
                 nc.tensor.matmul_mx(
                     out=kv[:],
@@ -312,6 +322,15 @@ def tile_mla_pb_t_kernel(tc, X, Wkv_down, bkv_down, Wkv_up, bkv_up, out_0, out_1
                     start=True,
                     stop=True,
                 )
+                kvs.append(kv)
+            st[("u", i)] = kvs
+
+        def finish(i):
+            G, half = divmod(i, 2)
+            key_sb, val_sb = st[("o", G)]
+            buv = bias_sb[:, 640:1152].rearrange("p (h x d) -> p h x d", h=4, x=2, d=64)
+            for a, kv in enumerate(st.pop(("u", i))):
+                t = 2 * half + a
                 kvv = kv[:].rearrange("p (h x d) -> p h x d", h=4, x=2, d=64)
                 nc.vector.tensor_tensor(out=key_sb[:, :, t, 0:64], in0=kvv[:, :, 0, :], in1=buv[:, :, 0, :], op=ALU.add)
                 nc.vector.tensor_tensor(out=val_sb[:, :, t, :], in0=kvv[:, :, 1, :], in1=buv[:, :, 1, :], op=ALU.add)
@@ -332,15 +351,31 @@ def tile_mla_pb_t_kernel(tc, X, Wkv_down, bkv_down, Wkv_up, bkv_up, out_0, out_1
             if half == 1:
                 st.pop(("o", G))
 
-        for i in range(NPAIR + 4):
-            if i < NPAIR:
-                stage_a(i)
-            if 0 <= i - 3 < NPAIR:
-                stage_e(i - 3)
-                stage_r(i - 3)
-            if i == 2:
+        turn_x(0)
+        for s in range(NPAIR + 3):
+            if 0 <= s - 2 < NPAIR:
+                scale_n(s - 2, 1)
+            if 0 <= s - 1 < NPAIR:
+                add_bias(s - 1)
+            if s < NPAIR:
+                quantise_x(s)
+            if s == 0:
+                wrap_turns()
+            if 0 <= s - 2 < NPAIR:
+                turn_n(s - 2)
+            if s + 1 < NPAIR:
+                turn_x(s + 1)
+            if s == 1:
+                make_tables()
                 prep_wu()
-            if 0 <= i - 1 < NPAIR:
-                stage_c(i - 1)
-            if 0 <= i - 4 < NPAIR:
-                stage_g(i - 4)
+            if 0 <= s - 1 < NPAIR:
+                norm(s - 1)
+                scale_n(s - 1, 0)
+                rotate(s - 1)
+            if 0 <= s - 3:
+                up(s - 3)
+                finish(s - 3)
+            if s < NPAIR:
+                down(s)
+            if s == 1:
+                spread_bias(nc.scalar.copy, ps_kv, "kv", 640, 1152)

@@ -188,7 +188,8 @@ def tile_mla_pb_t_kernel(tc, X, Wkv_down, bkv_down, Wkv_up, bkv_up, out_0, out_1
             xg = xg_pool.tile([P, 2048], BF16, name="xg", align_bytes=64)
             xgw = xg[:].bitcast(F32)
             for a, xt in enumerate(st.pop(("xt", i))):
-                nc.scalar.copy(
+                eng_copy = nc.vector.tensor_copy if a == 1 and i % 2 == 1 else nc.scalar.copy
+                eng_copy(
                     out=xgw[:, a * 512 : (a + 1) * 512].rearrange("q (g t u) -> q g t u", g=2, t=P, u=2),
                     in_=xt[:].rearrange("q (g u) t -> q g t u", g=2, u=2),
                 )
@@ -203,9 +204,9 @@ def tile_mla_pb_t_kernel(tc, X, Wkv_down, bkv_down, Wkv_up, bkv_up, out_0, out_1
             l_pss = []
             for a in range(2):
                 l_ps = ps_l.tile([P, 512], F32, name="l_ps")
-                for g in range(2):
-                    o = a * 256 + g * P
-                    for out, lo, hi in ((l_ps[:], 128, 640), (r_ps[:, a, :], 0, 128)):
+                for out, lo, hi in ((l_ps[:], 128, 640), (r_ps[:, a, :], 0, 128)):
+                    for g in range(2):
+                        o = a * 256 + g * P
                         nc.tensor.matmul_mx(
                             out=out,
                             lhsT=xc[:, o : o + P].bitcast(FP8X4),
@@ -218,13 +219,16 @@ def tile_mla_pb_t_kernel(tc, X, Wkv_down, bkv_down, Wkv_up, bkv_up, out_0, out_1
                 l_pss.append(l_ps)
             st[("d", i)] = (l_pss, r_ps)
 
-        def add_bias(i):
-            l_pss, r_ps = st.pop(("d", i))
+        def add_bias_l(i):
             l_sbs = []
-            for l_ps in l_pss:
+            for l_ps in st[("d", i)][0]:
                 l_sb = l_pool.tile([P, 512], F32, name="l_sb")
                 nc.vector.tensor_tensor(out=l_sb[:], in0=l_ps[:], in1=bias_sb[:, 128:640], op=ALU.add)
                 l_sbs.append(l_sb)
+            st[("l", i)] = l_sbs
+
+        def add_bias_r(i):
+            r_ps = st.pop(("d", i))[1]
             r_sb = rkeep.tile([P, 2, P], F32, name="r_sb")
             nc.vector.tensor_tensor(
                 out=r_sb[:],
@@ -232,7 +236,6 @@ def tile_mla_pb_t_kernel(tc, X, Wkv_down, bkv_down, Wkv_up, bkv_up, out_0, out_1
                 in1=bias_sb[:, 0:128].unsqueeze(1).to_broadcast([P, 2, P]),
                 op=ALU.add,
             )
-            st[("l", i)] = l_sbs
             st[("r", i)] = r_sb
 
         def norm(i):
@@ -248,16 +251,13 @@ def tile_mla_pb_t_kernel(tc, X, Wkv_down, bkv_down, Wkv_up, bkv_up, out_0, out_1
             )
             st[("s", i)] = rstd
 
-        def scale_n(i, a):
-            if a == 0:
-                st[("n", i)] = n_pool.tile([P, 2, 512], BF16, name="n_bf")
-            n_bf = st[("n", i)]
-            l_sb = st[("l", i)][a]
-            rstd = st[("s", i)]
-            if a == 0 or i % 3 == 0:
-                nc.scalar.activation(out=n_bf[:, a, :], in_=l_sb[:], func=AF.Copy, scale=rstd[:, a : a + 1])
-            else:
-                nc.vector.tensor_scalar_mul(out=n_bf[:, a, :], in0=l_sb[:], scalar1=rstd[:, a : a + 1])
+        def scale_n(i):
+            l_sbs = st.pop(("l", i))
+            rstd = st.pop(("s", i))
+            n_bf = n_pool.tile([P, 2, 512], BF16, name="n_bf")
+            for a in range(2):
+                nc.scalar.activation(out=n_bf[:, a, :], in_=l_sbs[a][:], func=AF.Copy, scale=rstd[:, a : a + 1])
+            st[("n", i)] = n_bf
 
         def rotate(i):
             G, half = divmod(i, 2)
@@ -353,10 +353,8 @@ def tile_mla_pb_t_kernel(tc, X, Wkv_down, bkv_down, Wkv_up, bkv_up, out_0, out_1
 
         turn_x(0)
         for s in range(NPAIR + 3):
-            if 0 <= s - 2 < NPAIR:
-                scale_n(s - 2, 1)
             if 0 <= s - 1 < NPAIR:
-                add_bias(s - 1)
+                add_bias_l(s - 1)
             if s < NPAIR:
                 quantise_x(s)
             if s == 0:
@@ -370,7 +368,8 @@ def tile_mla_pb_t_kernel(tc, X, Wkv_down, bkv_down, Wkv_up, bkv_up, out_0, out_1
                 prep_wu()
             if 0 <= s - 1 < NPAIR:
                 norm(s - 1)
-                scale_n(s - 1, 0)
+                scale_n(s - 1)
+                add_bias_r(s - 1)
                 rotate(s - 1)
             if 0 <= s - 3:
                 up(s - 3)

@@ -110,17 +110,17 @@ def tile_mla_pb_t_kernel(tc, X, Wkv_down, bkv_down, Wkv_up, bkv_up, out_0, out_1
         g_scale(turns[:, 1], turns[:, 0], 1.0, 0.25)
         whole = const.tile([P, 2, 8, 64], I32, name="whole")
         frac = const.tile([P, 2, 8, 64], F32, name="frac")
-        cos_t = const.tile([P, 8, 64], F32, name="cos_t")
-        sin_t = const.tile([P, 8, 2, 64], F32, name="sin_t")
+        table = const.tile([P, 2, 8, 2, 64], F32, name="table")
 
         def wrap_turns():
             nc.vector.tensor_copy(out=whole[:], in_=turns[:])
             nc.vector.tensor_tensor(out=frac[:], in0=turns[:], in1=whole[:], op=ALU.subtract)
 
         def make_tables():
-            nc.scalar.activation(out=sin_t[:, :, 1, :], in_=frac[:, 0], func=AF.Sin, scale=TWO_PI)
-            nc.scalar.activation(out=cos_t[:], in_=frac[:, 1], func=AF.Sin, scale=TWO_PI)
-            g_scale(sin_t[:, :, 0, :], sin_t[:, :, 1, :], -1.0)
+            nc.scalar.activation(out=table[:, 1, :, 0, :], in_=frac[:, 0], func=AF.Sin, scale=TWO_PI)
+            nc.scalar.activation(out=table[:, 0, :, 0, :], in_=frac[:, 1], func=AF.Sin, scale=TWO_PI)
+            g_scale(table[:, 1, :, 1, :], table[:, 1, :, 0, :], -1.0)
+            g_scale(table[:, 0, :, 1, :], table[:, 0, :, 0, :], 1.0)
 
         bias_sb = const.tile([P, 1152], F32, name="bias_sb")
 
@@ -188,8 +188,7 @@ def tile_mla_pb_t_kernel(tc, X, Wkv_down, bkv_down, Wkv_up, bkv_up, out_0, out_1
             xg = xg_pool.tile([P, 2048], BF16, name="xg", align_bytes=64)
             xgw = xg[:].bitcast(F32)
             for a, xt in enumerate(st.pop(("xt", i))):
-                eng_copy = nc.vector.tensor_copy if a == 1 and i % 2 == 1 else nc.scalar.copy
-                eng_copy(
+                nc.scalar.copy(
                     out=xgw[:, a * 512 : (a + 1) * 512].rearrange("q (g t u) -> q g t u", g=2, t=P, u=2),
                     in_=xt[:].rearrange("q (g u) t -> q g t u", g=2, u=2),
                 )
@@ -269,26 +268,25 @@ def tile_mla_pb_t_kernel(tc, X, Wkv_down, bkv_down, Wkv_up, bkv_up, out_0, out_1
             key_sb, val_sb = st[("o", G)]
             t0 = 2 * half
             gt = (G % 2) * 4 + t0
-            rv = r_sb[:].rearrange("p a (h d) -> p a h d", h=2)
-            m1 = rope.tile([P, 2, 2, 64], F32, name="m1")
-            m2 = rope.tile([P, 2, 2, 64], F32, name="m2")
+            both = rope.tile([P, 2, 2, 2, 64], F32, name="both")
+            fl = "p x a h d -> p x (a h d)"
             nc.gpsimd.tensor_tensor(
-                out=m1[:],
-                in0=rv,
-                in1=cos_t[:, gt : gt + 2, :].unsqueeze(2).to_broadcast([P, 2, 2, 64]),
+                out=both[:].rearrange(fl),
+                in0=r_sb[:].rearrange("p a c -> p (a c)").unsqueeze(1).to_broadcast([P, 2, 2 * P]),
+                in1=table[:, :, gt : gt + 2].rearrange(fl),
                 op=ALU.mult,
             )
             nc.gpsimd.tensor_tensor(
-                out=m2[:], in0=rv[:, :, ::-1, :], in1=sin_t[:, gt : gt + 2, :, :], op=ALU.mult
-            )
-            first = key_sb[:, 0, t0 : t0 + 2, 64:192]
-            nc.gpsimd.tensor_tensor(
-                out=first,
-                in0=m1[:].rearrange("p a h d -> p a (h d)"),
-                in1=m2[:].rearrange("p a h d -> p a (h d)"),
+                out=key_sb[:, 0, t0 : t0 + 2, 64:192].rearrange("p a (h d) -> p a h d", h=2),
+                in0=both[:, 0],
+                in1=both[:, 1, :, ::-1, :],
                 op=ALU.add,
             )
-            g_scale(key_sb[:, 1:4, t0 : t0 + 2, 64:192], first.unsqueeze(1).to_broadcast([P, 3, 2, P]), 1.0)
+
+        def spread_heads(i):
+            G, half = divmod(i, 2)
+            rope_cols = st[("o", G)][0][:, :, 2 * half : 2 * half + 2, 64:192]
+            nc.vector.tensor_copy(out=rope_cols[:, 1:4], in_=rope_cols[:, 0:1].to_broadcast([P, 3, 2, P]))
 
         def turn_n(i):
             n_bf = st.pop(("n", i))
@@ -361,6 +359,7 @@ def tile_mla_pb_t_kernel(tc, X, Wkv_down, bkv_down, Wkv_up, bkv_up, out_0, out_1
                 wrap_turns()
             if 0 <= s - 2 < NPAIR:
                 turn_n(s - 2)
+                spread_heads(s - 2)
             if s + 1 < NPAIR:
                 turn_x(s + 1)
             if s == 1:

@@ -26,10 +26,10 @@ def tile_mla_pb_t_kernel(tc, X, Wkv_down, bkv_down, Wkv_up, bkv_up, out_0, out_1
     nc = tc.nc
     with ExitStack() as ctx:
         const = ctx.enter_context(tc.tile_pool(name="const", bufs=1))
-        xres = ctx.enter_context(tc.tile_pool(name="xres", bufs=NQUAD))
-        xg_pool = ctx.enter_context(tc.tile_pool(name="xg", bufs=3))
+        xres = ctx.enter_context(tc.tile_pool(name="xres", bufs=6))
+        xg_pool = ctx.enter_context(tc.tile_pool(name="xg", bufs=4))
         l_pool = ctx.enter_context(tc.tile_pool(name="lp", bufs=6))
-        n_pool = ctx.enter_context(tc.tile_pool(name="np", bufs=3))
+        n_pool = ctx.enter_context(tc.tile_pool(name="np", bufs=4))
         small = ctx.enter_context(tc.tile_pool(name="small", bufs=4))
         rope = ctx.enter_context(tc.tile_pool(name="rope", bufs=2))
         rkeep = ctx.enter_context(tc.tile_pool(name="rkeep", bufs=4))
@@ -184,14 +184,17 @@ def tile_mla_pb_t_kernel(tc, X, Wkv_down, bkv_down, Wkv_up, bkv_up, out_0, out_1
                 xts.append(xt)
             st[("xt", i)] = xts
 
+        def copy_x(i, a):
+            if a == 0:
+                st[("xg", i)] = xg_pool.tile([P, 2048], BF16, name="xg", align_bytes=64)
+            xgw = st[("xg", i)][:].bitcast(F32)
+            nc.scalar.copy(
+                out=xgw[:, a * 512 : (a + 1) * 512].rearrange("q (g t u) -> q g t u", g=2, t=P, u=2),
+                in_=st[("xt", i)][a][:].rearrange("q (g u) t -> q g t u", g=2, u=2),
+            )
+
         def quantise_x(i):
-            xg = xg_pool.tile([P, 2048], BF16, name="xg", align_bytes=64)
-            xgw = xg[:].bitcast(F32)
-            for a, xt in enumerate(st.pop(("xt", i))):
-                nc.scalar.copy(
-                    out=xgw[:, a * 512 : (a + 1) * 512].rearrange("q (g t u) -> q g t u", g=2, t=P, u=2),
-                    in_=xt[:].rearrange("q (g u) t -> q g t u", g=2, u=2),
-                )
+            xg = st.pop(("xg", i))
             xc = xg_pool.tile([P, 512], U32, name="xc", align_bytes=64)
             xs = xg_pool.tile([P, 512], U8, name="xs", align_bytes=64)
             nc.vector.quantize_mx(out=xc[:].bitcast(FP8X4), scales=xs[:], in_=xg[:])
@@ -237,13 +240,17 @@ def tile_mla_pb_t_kernel(tc, X, Wkv_down, bkv_down, Wkv_up, bkv_up, out_0, out_1
             )
             st[("r", i)] = r_sb
 
-        def norm(i):
+        def square(i):
             ss = small.tile([P, 2], F32, name="ss")
             for a in range(2):
                 junk = small.tile([P, 512], BF16, name="junk")
                 nc.scalar.activation(
                     out=junk[:], in_=st[("l", i)][a][:], func=AF.Square, accum_out=ss[:, a : a + 1]
                 )
+            st[("ss", i)] = ss
+
+        def find_rstd(i):
+            ss = st.pop(("ss", i))
             rstd = small.tile([P, 2], F32, name="rstd")
             nc.scalar.activation(
                 out=rstd[:], in_=ss[:], func=AF.Abs_reciprocal_sqrt, scale=1.0 / 512.0, bias=eps_t[:, 0:1]
@@ -296,11 +303,18 @@ def tile_mla_pb_t_kernel(tc, X, Wkv_down, bkv_down, Wkv_up, bkv_up, out_0, out_1
                 for u in range(2):
                     c0 = a * 256 + u * P
                     nc.tensor.transpose(nt[:, a, u, :], nw[:, c0 : c0 + P], ident_f[:])
+            st[("nt", i)] = nt
+
+        def copy_n(i):
             ng = n_pool.tile([P, 1024], BF16, name="ng", align_bytes=64)
             nc.scalar.copy(
                 out=ng[:].bitcast(F32).rearrange("p (a t u) -> p a t u", a=2, t=P, u=2),
-                in_=nt[:].rearrange("p a u t -> p a t u"),
+                in_=st.pop(("nt", i))[:].rearrange("p a u t -> p a t u"),
             )
+            st[("ng", i)] = ng
+
+        def quantise_n(i):
+            ng = st.pop(("ng", i))
             ncd = n_pool.tile([P, 256], U32, name="ncd", align_bytes=64)
             nsc = n_pool.tile([P, 256], U8, name="nsc", align_bytes=64)
             nc.vector.quantize_mx(out=ncd[:].bitcast(FP8X4), scales=nsc[:], in_=ng[:])
@@ -349,31 +363,52 @@ def tile_mla_pb_t_kernel(tc, X, Wkv_down, bkv_down, Wkv_up, bkv_up, out_0, out_1
             if half == 1:
                 st.pop(("o", G))
 
-        turn_x(0)
+        for i in range(2):
+            turn_x(i)
+            copy_x(i, 0)
+            copy_x(i, 1)
+            quantise_x(i)
+        wrap_turns()
+        make_tables()
         for s in range(NPAIR + 3):
-            if 0 <= s - 1 < NPAIR:
-                add_bias_l(s - 1)
-            if s < NPAIR:
-                quantise_x(s)
-            if s == 0:
-                wrap_turns()
-            if 0 <= s - 2 < NPAIR:
-                turn_n(s - 2)
-                spread_heads(s - 2)
-            if s + 1 < NPAIR:
-                turn_x(s + 1)
-            if s == 1:
-                make_tables()
-                prep_wu()
-            if 0 <= s - 1 < NPAIR:
-                norm(s - 1)
-                scale_n(s - 1)
-                add_bias_r(s - 1)
-                rotate(s - 1)
+            live = s < NPAIR
+            ahead = s + 3 if s > 0 else 2
+            if live:
+                down(s)
             if 0 <= s - 3:
                 up(s - 3)
+            if live:
+                add_bias_l(s)
+                add_bias_r(s)
+                rotate(s)
+            if ahead < NPAIR:
+                turn_x(ahead)
+            if 0 <= s - 1 < NPAIR:
+                turn_n(s - 1)
+            if live:
+                square(s)
+            if ahead < NPAIR:
+                copy_x(ahead, 0)
+            if 0 <= s - 1 < NPAIR:
+                copy_n(s - 1)
+            if live:
+                find_rstd(s)
+            if ahead < NPAIR:
+                copy_x(ahead, 1)
+            if live:
+                scale_n(s)
+            if s == 0:
+                turn_x(3)
+                copy_x(3, 0)
+                copy_x(3, 1)
+            if s + 2 < NPAIR:
+                quantise_x(s + 2)
+            if s == 1:
+                prep_wu()
+            if 0 <= s - 2 < NPAIR:
+                quantise_n(s - 2)
+                spread_heads(s - 2)
+            if 0 <= s - 3:
                 finish(s - 3)
-            if s < NPAIR:
-                down(s)
             if s == 1:
                 spread_bias(nc.scalar.copy, ps_kv, "kv", 640, 1152)

@@ -17,6 +17,7 @@ ALU = mybir.AluOpType
 
 P = 128
 NQUAD = 8
+NXBUF = 6
 NPAIR = 16
 EPS = 1e-6
 TWO_PI = 2.0 * math.pi
@@ -26,7 +27,7 @@ def tile_mla_pb_t_kernel(tc, X, Wkv_down, bkv_down, Wkv_up, bkv_up, out_0, out_1
     nc = tc.nc
     with ExitStack() as ctx:
         const = ctx.enter_context(tc.tile_pool(name="const", bufs=1))
-        xres = ctx.enter_context(tc.tile_pool(name="xres", bufs=6))
+        xres = ctx.enter_context(tc.tile_pool(name="xres", bufs=NXBUF))
         xg_pool = ctx.enter_context(tc.tile_pool(name="xg", bufs=4))
         l_pool = ctx.enter_context(tc.tile_pool(name="lp", bufs=6))
         n_pool = ctx.enter_context(tc.tile_pool(name="np", bufs=4))
@@ -48,34 +49,41 @@ def tile_mla_pb_t_kernel(tc, X, Wkv_down, bkv_down, Wkv_up, bkv_up, out_0, out_1
         wu_raw = const.tile([P, 4, 512], BF16, name="wu_raw")
         x_sb = []
 
-        def load_x(G, pieces):
-            b, g = divmod(G, 2)
+        def open_x(G):
             x_sb.append(xres.tile([P, 4096], BF16, name="x_sb"))
+
+        def load_x(G, lo, hi):
+            b, g = divmod(G, 2)
             src = X[b, g * 512 : (g + 1) * 512, :].rearrange("(p t) k -> p t k", t=4)
             dst = x_sb[G][:].rearrange("p (t k) -> p t k", t=4)
-            w = 4 // pieces
-            for k in range(pieces):
-                nc.sync.dma_start(out=dst[:, k * w : (k + 1) * w, :], in_=src[:, k * w : (k + 1) * w, :])
+            nc.sync.dma_start(out=dst[:, lo:hi, :], in_=src[:, lo:hi, :])
 
         brow = const.tile([P, 1152], BF16, name="brow")
         nc.vector.memset(brow[:].bitcast(I32), 0)
+        open_x(0)
+        load_x(0, 0, 1)
+        load_x(0, 1, 2)
         nc.sync.dma_start(out=wd_dst[:, 0:2, :], in_=wd_src[:, 0:2, :])
+        nc.sync.dma_start(out=wd_dst[:, 2:4, :], in_=wd_src[:, 2:4, :])
         nc.sync.dma_start(out=brow[0:1, 0:640], in_=bkv_down.rearrange("(o n) -> o n", o=1))
         nc.sync.dma_start(out=brow[0:1, 640:1152], in_=bkv_up.rearrange("(o n) -> o n", o=1))
-        nc.sync.dma_start(out=wd_dst[:, 2:4, :], in_=wd_src[:, 2:4, :])
-        load_x(0, 4)
+        load_x(0, 2, 4)
         nc.sync.dma_start(
             out=wu_raw[:].rearrange("p (u e) n -> p u (e n)", u=2),
             in_=Wkv_up.rearrange("(u p e) n -> p u (e n)", u=2, p=P, e=2),
         )
-        for G in range(1, NQUAD):
-            load_x(G, 1)
+        for G in range(1, NXBUF):
+            open_x(G)
+            load_x(G, 0, 4)
 
         ones = const.tile([P, P], BF16, name="ones")
         nc.vector.memset(ones[:], 1.0)
         eps_t = const.tile([P, 1], F32, name="eps_t")
         nc.vector.memset(eps_t[:], 0.0)
         nc.vector.tensor_scalar_add(out=eps_t[:], in0=eps_t[:], scalar1=EPS)
+
+        warm = const.tile([P, 2], F32, name="warm")
+        nc.scalar.activation(out=warm[:, 0:1], in_=eps_t[:], func=AF.Sin)
 
         ident_f = const.tile([P, P], F32, name="ident_f")
         make_identity(nc, ident_f[:])
@@ -88,39 +96,50 @@ def tile_mla_pb_t_kernel(tc, X, Wkv_down, bkv_down, Wkv_up, bkv_up, out_0, out_1
             channel_multiplier=4,
             allow_small_or_imprecise_dtypes=True,
         )
-        tf = const.tile([P, 64], F32, name="tf")
-        nc.gpsimd.memset(tf[:, 0:1], 1.0)
+        rows = const.tile([P, 2, 8], F32, name="rows")
+        nc.vector.memset(rows[:, :, 0:1], 1.0)
+        nc.vector.tensor_scalar_mul(out=rows[:, 0, 0:1], in0=rows[:, 0, 0:1], scalar1=1.0 / TWO_PI)
+        ratio = 10000.0 ** (-1.0 / 64.0)
+        for n in (1, 2, 4):
+            for k, step in ((1, 1), (0, 8)):
+                nc.vector.tensor_scalar_mul(
+                    out=rows[:, k, n : 2 * n], in0=rows[:, k, 0:n], scalar1=ratio ** (n * step)
+                )
+        tf = const.tile([P, 8, 8], F32, name="tf")
+        nc.vector.tensor_tensor(
+            out=tf[:],
+            in0=rows[:, 0].unsqueeze(2).to_broadcast([P, 8, 8]),
+            in1=rows[:, 1].unsqueeze(1).to_broadcast([P, 8, 8]),
+            op=ALU.mult,
+        )
+        turns = const.tile([P, 8, 64], F32, name="turns")
+        nc.vector.tensor_tensor(
+            out=turns[:],
+            in0=pos[:].unsqueeze(2).to_broadcast([P, 8, 64]),
+            in1=tf[:].rearrange("p a b -> p (a b)").unsqueeze(1).to_broadcast([P, 8, 64]),
+            op=ALU.mult,
+        )
 
         def g_scale(out, in_, factor, offset=0.0):
             nc.gpsimd.tensor_scalar(out=out, in0=in_, scalar1=factor, scalar2=offset, op0=ALU.mult, op1=ALU.add)
 
-        g_scale(tf[:, 0:1], tf[:, 0:1], 1.0 / TWO_PI)
-        ratio = 10000.0 ** (-1.0 / 64.0)
-        n = 1
-        while n < 64:
-            g_scale(tf[:, n : 2 * n], tf[:, 0:n], ratio**n)
-            n *= 2
-        turns = const.tile([P, 2, 8, 64], F32, name="turns")
-        nc.gpsimd.tensor_tensor(
-            out=turns[:, 0],
-            in0=pos[:].unsqueeze(2).to_broadcast([P, 8, 64]),
-            in1=tf[:].unsqueeze(1).to_broadcast([P, 8, 64]),
-            op=ALU.mult,
-        )
-        g_scale(turns[:, 1], turns[:, 0], 1.0, 0.25)
-        whole = const.tile([P, 2, 8, 64], I32, name="whole")
-        frac = const.tile([P, 2, 8, 64], F32, name="frac")
+        whole = const.tile([P, 8, 64], I32, name="whole")
+        frac = const.tile([P, 8, 64], F32, name="frac")
+        half_sin = const.tile([P, 8, 64], F32, name="half_sin")
         table = const.tile([P, 2, 8, 2, 64], F32, name="table")
 
-        def wrap_turns():
-            nc.vector.tensor_copy(out=whole[:], in_=turns[:])
-            nc.vector.tensor_tensor(out=frac[:], in0=turns[:], in1=whole[:], op=ALU.subtract)
+        nc.vector.tensor_copy(out=whole[:], in_=turns[:])
+        nc.vector.tensor_tensor(out=frac[:], in0=turns[:], in1=whole[:], op=ALU.subtract)
 
-        def make_tables():
-            nc.scalar.activation(out=table[:, 1, :, 0, :], in_=frac[:, 0], func=AF.Sin, scale=TWO_PI)
-            nc.scalar.activation(out=table[:, 0, :, 0, :], in_=frac[:, 1], func=AF.Sin, scale=TWO_PI)
+        def find_sines():
+            nc.scalar.activation(out=half_sin[:], in_=frac[:], func=AF.Sin, scale=0.5 * TWO_PI)
+            nc.scalar.activation(out=table[:, 1, :, 0, :], in_=frac[:], func=AF.Sin, scale=TWO_PI)
+
+        def finish_tables():
+            nc.scalar.activation(out=half_sin[:], in_=half_sin[:], func=AF.Square)
+            g_scale(table[:, 0, :, 0, :], half_sin[:], -2.0, 1.0)
+            g_scale(table[:, 0, :, 1, :], half_sin[:], -2.0, 1.0)
             g_scale(table[:, 1, :, 1, :], table[:, 1, :, 0, :], -1.0)
-            g_scale(table[:, 0, :, 1, :], table[:, 0, :, 0, :], 1.0)
 
         bias_sb = const.tile([P, 1152], F32, name="bias_sb")
 
@@ -146,25 +165,17 @@ def tile_mla_pb_t_kernel(tc, X, Wkv_down, bkv_down, Wkv_up, bkv_up, out_0, out_1
                 in_=wdg[:, g, lo:hi, :].rearrange("q c j -> q (c j)"),
             )
 
-        for g in range(2):
-            regroup_wd(nc.vector.tensor_copy, g, 128, 512)
-            regroup_wd(nc.scalar.copy, g, 512, 640)
-            regroup_wd(nc.scalar.copy, g, 0, 128)
-            if g == 0:
-                spread_bias(nc.vector.tensor_copy, ps_l, "l_ps", 128, 640)
-                spread_bias(nc.scalar.copy, ps_l, "l_ps", 0, 128)
-        for g in range(2):
-            quantise_wd(g, 128, 640)
-            quantise_wd(g, 0, 128)
         wug = const.tile([P, 512, 4], BF16, name="wug", align_bytes=64)
         wuc = const.tile([P, 512], U32, name="wuc", align_bytes=64)
         wus = const.tile([P, 512], U8, name="wus", align_bytes=64)
 
-        def prep_wu():
+        def regroup_wu(lo, hi):
             nc.vector.tensor_copy(
-                out=wug[:].rearrange("q (c i) j -> q c j i", i=4),
-                in_=wu_raw[:].rearrange("q j (c i) -> q c j i", i=4),
+                out=wug[:, lo:hi].rearrange("q (c i) j -> q c j i", i=4),
+                in_=wu_raw[:, :, lo:hi].rearrange("q j (c i) -> q c j i", i=4),
             )
+
+        def quantise_wu():
             nc.vector.quantize_mx(
                 out=wuc[:].bitcast(FP8X4), scales=wus[:], in_=wug[:].rearrange("q c j -> q (c j)")
             )
@@ -240,30 +251,37 @@ def tile_mla_pb_t_kernel(tc, X, Wkv_down, bkv_down, Wkv_up, bkv_up, out_0, out_1
             )
             st[("r", i)] = r_sb
 
-        def square(i):
-            ss = small.tile([P, 2], F32, name="ss")
-            for a in range(2):
+        def square(i, tiles):
+            if 0 in tiles:
+                st[("ss", i)] = small.tile([P, 2], F32, name="ss")
+            ss = st[("ss", i)]
+            for a in tiles:
                 junk = small.tile([P, 512], BF16, name="junk")
                 nc.scalar.activation(
                     out=junk[:], in_=st[("l", i)][a][:], func=AF.Square, accum_out=ss[:, a : a + 1]
                 )
-            st[("ss", i)] = ss
 
-        def find_rstd(i):
-            ss = st.pop(("ss", i))
-            rstd = small.tile([P, 2], F32, name="rstd")
+        def find_rstd(i, tiles):
+            if 0 in tiles:
+                st[("s", i)] = small.tile([P, 2], F32, name="rstd")
+            cols = slice(tiles[0], tiles[-1] + 1)
             nc.scalar.activation(
-                out=rstd[:], in_=ss[:], func=AF.Abs_reciprocal_sqrt, scale=1.0 / 512.0, bias=eps_t[:, 0:1]
+                out=st[("s", i)][:, cols],
+                in_=st[("ss", i)][:, cols],
+                func=AF.Abs_reciprocal_sqrt,
+                scale=1.0 / 512.0,
+                bias=eps_t[:, 0:1],
             )
-            st[("s", i)] = rstd
 
-        def scale_n(i):
-            l_sbs = st.pop(("l", i))
-            rstd = st.pop(("s", i))
-            n_bf = n_pool.tile([P, 2, 512], BF16, name="n_bf")
-            for a in range(2):
-                nc.scalar.activation(out=n_bf[:, a, :], in_=l_sbs[a][:], func=AF.Copy, scale=rstd[:, a : a + 1])
-            st[("n", i)] = n_bf
+        def scale_n(i, tiles):
+            if 0 in tiles:
+                st[("n", i)] = n_pool.tile([P, 2, 512], BF16, name="n_bf")
+            n_bf = st[("n", i)]
+            rstd = st[("s", i)]
+            for a in tiles:
+                nc.scalar.activation(
+                    out=n_bf[:, a, :], in_=st[("l", i)][a][:], func=AF.Copy, scale=rstd[:, a : a + 1]
+                )
 
         def rotate(i):
             G, half = divmod(i, 2)
@@ -295,35 +313,39 @@ def tile_mla_pb_t_kernel(tc, X, Wkv_down, bkv_down, Wkv_up, bkv_up, out_0, out_1
             rope_cols = st[("o", G)][0][:, :, 2 * half : 2 * half + 2, 64:192]
             nc.vector.tensor_copy(out=rope_cols[:, 1:4], in_=rope_cols[:, 0:1].to_broadcast([P, 3, 2, P]))
 
-        def turn_n(i):
-            n_bf = st.pop(("n", i))
-            nw = n_bf[:].rearrange("p a c -> p (a c)").bitcast(F32)
-            nt = ps_nt.tile([P, 2, 2, P], F32, name="nt")
-            for a in range(2):
+        def turn_n(i, tiles):
+            if 0 in tiles:
+                st[("nt", i)] = ps_nt.tile([P, 2, 2, P], F32, name="nt")
+            nt = st[("nt", i)]
+            nw = st[("n", i)][:].rearrange("p a c -> p (a c)").bitcast(F32)
+            for a in tiles:
                 for u in range(2):
                     c0 = a * 256 + u * P
                     nc.tensor.transpose(nt[:, a, u, :], nw[:, c0 : c0 + P], ident_f[:])
-            st[("nt", i)] = nt
 
-        def copy_n(i):
-            ng = n_pool.tile([P, 1024], BF16, name="ng", align_bytes=64)
+        def copy_n(i, tiles):
+            if 0 in tiles:
+                st[("ng", i)] = n_pool.tile([P, 1024], BF16, name="ng", align_bytes=64)
+            cols = slice(tiles[0], tiles[-1] + 1)
             nc.scalar.copy(
-                out=ng[:].bitcast(F32).rearrange("p (a t u) -> p a t u", a=2, t=P, u=2),
-                in_=st.pop(("nt", i))[:].rearrange("p a u t -> p a t u"),
+                out=st[("ng", i)][:].bitcast(F32).rearrange("p (a t u) -> p a t u", a=2, t=P, u=2)[:, cols],
+                in_=st[("nt", i)][:, cols].rearrange("p a u t -> p a t u"),
             )
-            st[("ng", i)] = ng
 
-        def quantise_n(i):
-            ng = st.pop(("ng", i))
-            ncd = n_pool.tile([P, 256], U32, name="ncd", align_bytes=64)
-            nsc = n_pool.tile([P, 256], U8, name="nsc", align_bytes=64)
-            nc.vector.quantize_mx(out=ncd[:].bitcast(FP8X4), scales=nsc[:], in_=ng[:])
-            st[("q", i)] = (ncd, nsc)
+        def quantise_n(i, tiles):
+            if 0 in tiles:
+                ncd = n_pool.tile([P, 256], U32, name="ncd", align_bytes=64)
+                nsc = n_pool.tile([P, 256], U8, name="nsc", align_bytes=64)
+                st[("q", i)] = (ncd, nsc)
+            ncd, nsc = st[("q", i)]
+            lo, hi = tiles[0] * P, (tiles[-1] + 1) * P
+            nc.vector.quantize_mx(
+                out=ncd[:, lo:hi].bitcast(FP8X4), scales=nsc[:, lo:hi], in_=st[("ng", i)][:, 4 * lo : 4 * hi]
+            )
 
-        def up(i):
-            ncd, nsc = st.pop(("q", i))
-            kvs = []
-            for a in range(2):
+        def up(i, tiles):
+            ncd, nsc = st[("q", i)]
+            for a in tiles:
                 kv = ps_kv.tile([P, 512], F32, name="kv")
                 nc.tensor.matmul_mx(
                     out=kv[:],
@@ -334,81 +356,114 @@ def tile_mla_pb_t_kernel(tc, X, Wkv_down, bkv_down, Wkv_up, bkv_up, out_0, out_1
                     start=True,
                     stop=True,
                 )
-                kvs.append(kv)
-            st[("u", i)] = kvs
+                st[("u", i, a)] = kv
 
-        def finish(i):
+        def finish(i, tiles):
             G, half = divmod(i, 2)
             key_sb, val_sb = st[("o", G)]
             buv = bias_sb[:, 640:1152].rearrange("p (h x d) -> p h x d", h=4, x=2, d=64)
-            for a, kv in enumerate(st.pop(("u", i))):
+            for a in tiles:
                 t = 2 * half + a
-                kvv = kv[:].rearrange("p (h x d) -> p h x d", h=4, x=2, d=64)
+                kvv = st[("u", i, a)][:].rearrange("p (h x d) -> p h x d", h=4, x=2, d=64)
                 nc.vector.tensor_tensor(out=key_sb[:, :, t, 0:64], in0=kvv[:, :, 0, :], in1=buv[:, :, 0, :], op=ALU.add)
                 nc.vector.tensor_tensor(out=val_sb[:, :, t, :], in0=kvv[:, :, 1, :], in1=buv[:, :, 1, :], op=ALU.add)
-            b, g = divmod(G, 2)
-            if G == NQUAD - 1:
-                lo, hi = 2 * half, 2 * half + 2
-            else:
-                lo, hi = 0, 4
-            if half == 1 or G == NQUAD - 1:
-                nc.sync.dma_start(
-                    out=out_0[b].rearrange("h (g p t) d -> g p h t d", g=2, p=P, t=4)[g][:, :, lo:hi, :],
-                    in_=key_sb[:, :, lo:hi, :],
-                )
-                nc.sync.dma_start(
-                    out=out_1[b].rearrange("h (g p t) d -> g p h t d", g=2, p=P, t=4)[g][:, :, lo:hi, :],
-                    in_=val_sb[:, :, lo:hi, :],
-                )
-            if half == 1:
-                st.pop(("o", G))
 
-        for i in range(2):
-            turn_x(i)
-            copy_x(i, 0)
-            copy_x(i, 1)
-            quantise_x(i)
-        wrap_turns()
-        make_tables()
-        for s in range(NPAIR + 3):
-            live = s < NPAIR
-            ahead = s + 3 if s > 0 else 2
-            if live:
-                down(s)
-            if 0 <= s - 3:
-                up(s - 3)
-            if live:
-                add_bias_l(s)
-                add_bias_r(s)
-                rotate(s)
+        def store(i, tiles):
+            G, half = divmod(i, 2)
+            key_sb, val_sb = st[("o", G)]
+            b, g = divmod(G, 2)
+            lo, hi = 2 * half + tiles[0], 2 * half + tiles[-1] + 1
+            for out, sb in ((out_0, key_sb), (out_1, val_sb)):
+                nc.sync.dma_start(
+                    out=out[b].rearrange("h (g p t) d -> g p h t d", g=2, p=P, t=4)[g][:, :, lo:hi, :],
+                    in_=sb[:, :, lo:hi, :],
+                )
+
+        vsplit = 128 + 384
+        both = (0, 1)
+        turn_x(0)
+        copy_x(0, 0)
+        copy_x(0, 1)
+        find_sines()
+        regroup_wd(nc.vector.tensor_copy, 0, 128, vsplit)
+        regroup_wd(nc.scalar.copy, 0, vsplit, 640)
+        quantise_x(0)
+        regroup_wd(nc.vector.tensor_copy, 1, 128, vsplit)
+        regroup_wd(nc.scalar.copy, 1, vsplit, 640)
+        nc.scalar.activation(out=warm[:, 1:2], in_=eps_t[:], func=AF.Abs_reciprocal_sqrt, bias=eps_t[:])
+        quantise_wd(0, 128, 640)
+        quantise_wd(1, 128, 640)
+        spread_bias(nc.scalar.copy, ps_l, "l_ps", 128, 640)
+        spread_bias(nc.scalar.copy, ps_l, "l_ps", 0, 128)
+        regroup_wd(nc.vector.tensor_copy, 0, 0, 128)
+        regroup_wd(nc.vector.tensor_copy, 1, 0, 128)
+        quantise_wd(0, 0, 128)
+        quantise_wd(1, 0, 128)
+        turn_x(1)
+        copy_x(1, 0)
+        copy_x(1, 1)
+        finish_tables()
+        for s in range(NPAIR):
+            ahead = s + 2
+            last = s == NPAIR - 1
+            if 0 <= s - 2:
+                quantise_n(s - 2, both)
+            down(s)
+            if 0 <= s - 2:
+                up(s - 2, both)
+            if s == 0:
+                quantise_x(1)
+                open_x(6)
+                load_x(6, 0, 4)
+            if s == 2:
+                open_x(7)
+                load_x(7, 0, 4)
+            add_bias_l(s)
+            add_bias_r(s)
+            rotate(s)
             if ahead < NPAIR:
                 turn_x(ahead)
-            if 0 <= s - 1 < NPAIR:
-                turn_n(s - 1)
-            if live:
-                square(s)
+            if 0 <= s - 1:
+                turn_n(s - 1, both)
+            square(s, (0,) if last else both)
             if ahead < NPAIR:
                 copy_x(ahead, 0)
-            if 0 <= s - 1 < NPAIR:
-                copy_n(s - 1)
-            if live:
-                find_rstd(s)
-            if ahead < NPAIR:
-                copy_x(ahead, 1)
-            if live:
-                scale_n(s)
-            if s == 0:
-                turn_x(3)
-                copy_x(3, 0)
-                copy_x(3, 1)
-            if s + 2 < NPAIR:
-                quantise_x(s + 2)
+            if 0 <= s - 1:
+                copy_n(s - 1, both)
+            if last:
+                find_rstd(s, (0,))
+                square(s, (1,))
+                scale_n(s, (0,))
+                find_rstd(s, (1,))
+                scale_n(s, (1,))
+            else:
+                find_rstd(s, both)
+                if ahead < NPAIR:
+                    copy_x(ahead, 1)
+                scale_n(s, both)
+            if s > 0 and s + 1 < NPAIR:
+                quantise_x(s + 1)
+            if s < 2:
+                regroup_wu(256 * s, 256 * s + 256)
             if s == 1:
-                prep_wu()
-            if 0 <= s - 2 < NPAIR:
-                quantise_n(s - 2)
-                spread_heads(s - 2)
-            if 0 <= s - 3:
-                finish(s - 3)
-            if s == 1:
+                quantise_wu()
                 spread_bias(nc.scalar.copy, ps_kv, "kv", 640, 1152)
+            if 0 <= s - 2:
+                spread_heads(s - 2)
+                finish(s - 2, both)
+                store(s - 2, both)
+        i = NPAIR - 1
+        quantise_n(i - 1, both)
+        up(i - 1, both)
+        for a in both:
+            turn_n(i, (a,))
+            copy_n(i, (a,))
+        spread_heads(i - 1)
+        finish(i - 1, both)
+        store(i - 1, both)
+        spread_heads(i)
+        for a in both:
+            quantise_n(i, (a,))
+            up(i, (a,))
+            finish(i, (a,))
+            store(i, (a,))

@@ -143,8 +143,8 @@ def tile_mla_pb_t_kernel(tc, X, Wkv_down, bkv_down, Wkv_up, bkv_up, out_0, out_1
 
         bias_sb = const.tile([P, 1152], F32, name="bias_sb")
 
-        def spread_bias(eng_copy, pool, tag, lo, hi):
-            bps = pool.tile([P, 512], F32, name="bps", tag=tag)
+        def spread_bias(eng_copy, lo, hi):
+            bps = ps_kv.tile([P, 512], F32, name="bps", tag="kv")
             nc.tensor.matmul(bps[:, 0 : hi - lo], lhsT=ones[:], rhs=brow[:, lo:hi], start=True, stop=True)
             eng_copy(out=bias_sb[:, lo:hi], in_=bps[:, 0 : hi - lo])
 
@@ -214,31 +214,28 @@ def tile_mla_pb_t_kernel(tc, X, Wkv_down, bkv_down, Wkv_up, bkv_up, out_0, out_1
         def down(i):
             xc, xs = st.pop(("x", i))
             r_ps = ps_r.tile([P, 2, P], F32, name="r_ps")
-            l_pss = []
-            for a in range(2):
-                l_ps = ps_l.tile([P, 512], F32, name="l_ps")
-                for out, lo, hi in ((l_ps[:], 128, 640), (r_ps[:, a, :], 0, 128)):
-                    for g in range(2):
-                        o = a * 256 + g * P
-                        nc.tensor.matmul_mx(
-                            out=out,
-                            lhsT=xc[:, o : o + P].bitcast(FP8X4),
-                            lhsT_scale=xs[:, o : o + P],
-                            rhs=wdc[:, g, lo:hi].bitcast(FP8X4),
-                            rhs_scale=wds[:, g, lo:hi],
-                            start=(g == 0),
-                            stop=(g == 1),
-                        )
-                l_pss.append(l_ps)
+            l_pss = [ps_l.tile([P, 512], F32, name="l_ps") for a in range(2)]
+            outs = [(a, l_pss[a][:], 128, 640) for a in range(2)] + [(a, r_ps[:, a, :], 0, 128) for a in range(2)]
+            for a, out, lo, hi in outs:
+                for g in range(2):
+                    o = a * 256 + g * P
+                    nc.tensor.matmul_mx(
+                        out=out,
+                        lhsT=xc[:, o : o + P].bitcast(FP8X4),
+                        lhsT_scale=xs[:, o : o + P],
+                        rhs=wdc[:, g, lo:hi].bitcast(FP8X4),
+                        rhs_scale=wds[:, g, lo:hi],
+                        start=(g == 0),
+                        stop=(g == 1),
+                    )
             st[("d", i)] = (l_pss, r_ps)
 
         def add_bias_l(i):
-            l_sbs = []
+            st[("l", i)] = []
             for l_ps in st[("d", i)][0]:
                 l_sb = l_pool.tile([P, 512], F32, name="l_sb")
                 nc.vector.tensor_tensor(out=l_sb[:], in0=l_ps[:], in1=bias_sb[:, 128:640], op=ALU.add)
-                l_sbs.append(l_sb)
-            st[("l", i)] = l_sbs
+                st[("l", i)].append(l_sb)
 
         def add_bias_r(i):
             r_ps = st.pop(("d", i))[1]
@@ -251,37 +248,33 @@ def tile_mla_pb_t_kernel(tc, X, Wkv_down, bkv_down, Wkv_up, bkv_up, out_0, out_1
             )
             st[("r", i)] = r_sb
 
-        def square(i, tiles):
-            if 0 in tiles:
-                st[("ss", i)] = small.tile([P, 2], F32, name="ss")
-            ss = st[("ss", i)]
-            for a in tiles:
+        def square(i):
+            ss = small.tile([P, 2], F32, name="ss")
+            for a in range(2):
                 junk = small.tile([P, 512], BF16, name="junk")
                 nc.scalar.activation(
                     out=junk[:], in_=st[("l", i)][a][:], func=AF.Square, accum_out=ss[:, a : a + 1]
                 )
+            st[("ss", i)] = ss
 
-        def find_rstd(i, tiles):
-            if 0 in tiles:
-                st[("s", i)] = small.tile([P, 2], F32, name="rstd")
-            cols = slice(tiles[0], tiles[-1] + 1)
+        def find_rstd(i):
+            rstd = small.tile([P, 2], F32, name="rstd")
             nc.scalar.activation(
-                out=st[("s", i)][:, cols],
-                in_=st[("ss", i)][:, cols],
+                out=rstd[:],
+                in_=st.pop(("ss", i))[:],
                 func=AF.Abs_reciprocal_sqrt,
                 scale=1.0 / 512.0,
                 bias=eps_t[:, 0:1],
             )
+            st[("s", i)] = rstd
 
-        def scale_n(i, tiles):
-            if 0 in tiles:
-                st[("n", i)] = n_pool.tile([P, 2, 512], BF16, name="n_bf")
-            n_bf = st[("n", i)]
-            rstd = st[("s", i)]
-            for a in tiles:
-                nc.scalar.activation(
-                    out=n_bf[:, a, :], in_=st[("l", i)][a][:], func=AF.Copy, scale=rstd[:, a : a + 1]
-                )
+        def scale_n(i):
+            l_sbs = st.pop(("l", i))
+            rstd = st.pop(("s", i))
+            n_bf = n_pool.tile([P, 2, 512], BF16, name="n_bf")
+            for a in range(2):
+                nc.scalar.activation(out=n_bf[:, a, :], in_=l_sbs[a][:], func=AF.Copy, scale=rstd[:, a : a + 1])
+            st[("n", i)] = n_bf
 
         def rotate(i):
             G, half = divmod(i, 2)
@@ -313,39 +306,33 @@ def tile_mla_pb_t_kernel(tc, X, Wkv_down, bkv_down, Wkv_up, bkv_up, out_0, out_1
             rope_cols = st[("o", G)][0][:, :, 2 * half : 2 * half + 2, 64:192]
             nc.vector.tensor_copy(out=rope_cols[:, 1:4], in_=rope_cols[:, 0:1].to_broadcast([P, 3, 2, P]))
 
-        def turn_n(i, tiles):
-            if 0 in tiles:
-                st[("nt", i)] = ps_nt.tile([P, 2, 2, P], F32, name="nt")
-            nt = st[("nt", i)]
-            nw = st[("n", i)][:].rearrange("p a c -> p (a c)").bitcast(F32)
-            for a in tiles:
+        def turn_n(i):
+            nw = st.pop(("n", i))[:].rearrange("p a c -> p (a c)").bitcast(F32)
+            nt = ps_nt.tile([P, 2, 2, P], F32, name="nt")
+            for a in range(2):
                 for u in range(2):
                     c0 = a * 256 + u * P
                     nc.tensor.transpose(nt[:, a, u, :], nw[:, c0 : c0 + P], ident_f[:])
+            st[("nt", i)] = nt
 
-        def copy_n(i, tiles):
-            if 0 in tiles:
-                st[("ng", i)] = n_pool.tile([P, 1024], BF16, name="ng", align_bytes=64)
-            cols = slice(tiles[0], tiles[-1] + 1)
+        def copy_n(i):
+            ng = n_pool.tile([P, 1024], BF16, name="ng", align_bytes=64)
             nc.scalar.copy(
-                out=st[("ng", i)][:].bitcast(F32).rearrange("p (a t u) -> p a t u", a=2, t=P, u=2)[:, cols],
-                in_=st[("nt", i)][:, cols].rearrange("p a u t -> p a t u"),
+                out=ng[:].bitcast(F32).rearrange("p (a t u) -> p a t u", a=2, t=P, u=2),
+                in_=st.pop(("nt", i))[:].rearrange("p a u t -> p a t u"),
             )
+            st[("ng", i)] = ng
 
-        def quantise_n(i, tiles):
-            if 0 in tiles:
-                ncd = n_pool.tile([P, 256], U32, name="ncd", align_bytes=64)
-                nsc = n_pool.tile([P, 256], U8, name="nsc", align_bytes=64)
-                st[("q", i)] = (ncd, nsc)
-            ncd, nsc = st[("q", i)]
-            lo, hi = tiles[0] * P, (tiles[-1] + 1) * P
-            nc.vector.quantize_mx(
-                out=ncd[:, lo:hi].bitcast(FP8X4), scales=nsc[:, lo:hi], in_=st[("ng", i)][:, 4 * lo : 4 * hi]
-            )
+        def quantise_n(i):
+            ncd = n_pool.tile([P, 256], U32, name="ncd", align_bytes=64)
+            nsc = n_pool.tile([P, 256], U8, name="nsc", align_bytes=64)
+            nc.vector.quantize_mx(out=ncd[:].bitcast(FP8X4), scales=nsc[:], in_=st.pop(("ng", i))[:])
+            st[("q", i)] = (ncd, nsc)
 
-        def up(i, tiles):
-            ncd, nsc = st[("q", i)]
-            for a in tiles:
+        def up(i):
+            ncd, nsc = st.pop(("q", i))
+            kvs = []
+            for a in range(2):
                 kv = ps_kv.tile([P, 512], F32, name="kv")
                 nc.tensor.matmul_mx(
                     out=kv[:],
@@ -356,23 +343,24 @@ def tile_mla_pb_t_kernel(tc, X, Wkv_down, bkv_down, Wkv_up, bkv_up, out_0, out_1
                     start=True,
                     stop=True,
                 )
-                st[("u", i, a)] = kv
+                kvs.append(kv)
+            st[("u", i)] = kvs
 
-        def finish(i, tiles):
+        def finish(i):
             G, half = divmod(i, 2)
             key_sb, val_sb = st[("o", G)]
             buv = bias_sb[:, 640:1152].rearrange("p (h x d) -> p h x d", h=4, x=2, d=64)
-            for a in tiles:
+            for a, kv in enumerate(st.pop(("u", i))):
                 t = 2 * half + a
-                kvv = st[("u", i, a)][:].rearrange("p (h x d) -> p h x d", h=4, x=2, d=64)
+                kvv = kv[:].rearrange("p (h x d) -> p h x d", h=4, x=2, d=64)
                 nc.vector.tensor_tensor(out=key_sb[:, :, t, 0:64], in0=kvv[:, :, 0, :], in1=buv[:, :, 0, :], op=ALU.add)
                 nc.vector.tensor_tensor(out=val_sb[:, :, t, :], in0=kvv[:, :, 1, :], in1=buv[:, :, 1, :], op=ALU.add)
 
-        def store(i, tiles):
+        def store(i):
             G, half = divmod(i, 2)
             key_sb, val_sb = st[("o", G)]
             b, g = divmod(G, 2)
-            lo, hi = 2 * half + tiles[0], 2 * half + tiles[-1] + 1
+            lo, hi = 2 * half, 2 * half + 2
             for out, sb in ((out_0, key_sb), (out_1, val_sb)):
                 nc.sync.dma_start(
                     out=out[b].rearrange("h (g p t) d -> g p h t d", g=2, p=P, t=4)[g][:, :, lo:hi, :],
@@ -380,7 +368,6 @@ def tile_mla_pb_t_kernel(tc, X, Wkv_down, bkv_down, Wkv_up, bkv_up, out_0, out_1
                 )
 
         vsplit = 128 + 384
-        both = (0, 1)
         turn_x(0)
         copy_x(0, 0)
         copy_x(0, 1)
@@ -393,8 +380,8 @@ def tile_mla_pb_t_kernel(tc, X, Wkv_down, bkv_down, Wkv_up, bkv_up, out_0, out_1
         nc.scalar.activation(out=warm[:, 1:2], in_=eps_t[:], func=AF.Abs_reciprocal_sqrt, bias=eps_t[:])
         quantise_wd(0, 128, 640)
         quantise_wd(1, 128, 640)
-        spread_bias(nc.scalar.copy, ps_l, "l_ps", 128, 640)
-        spread_bias(nc.scalar.copy, ps_l, "l_ps", 0, 128)
+        spread_bias(nc.scalar.copy, 128, 640)
+        spread_bias(nc.scalar.copy, 0, 128)
         regroup_wd(nc.vector.tensor_copy, 0, 0, 128)
         regroup_wd(nc.vector.tensor_copy, 1, 0, 128)
         quantise_wd(0, 0, 128)
@@ -403,67 +390,49 @@ def tile_mla_pb_t_kernel(tc, X, Wkv_down, bkv_down, Wkv_up, bkv_up, out_0, out_1
         copy_x(1, 0)
         copy_x(1, 1)
         finish_tables()
-        for s in range(NPAIR):
-            ahead = s + 2
-            last = s == NPAIR - 1
-            if 0 <= s - 2:
-                quantise_n(s - 2, both)
-            down(s)
-            if 0 <= s - 2:
-                up(s - 2, both)
-            if s == 0:
-                quantise_x(1)
-                open_x(6)
-                load_x(6, 0, 4)
+        quantise_x(1)
+        open_x(6)
+        load_x(6, 0, 4)
+        for s in range(NPAIR + 2):
+            live = s < NPAIR
             if s == 2:
                 open_x(7)
                 load_x(7, 0, 4)
-            add_bias_l(s)
-            add_bias_r(s)
-            rotate(s)
-            if ahead < NPAIR:
-                turn_x(ahead)
-            if 0 <= s - 1:
-                turn_n(s - 1, both)
-            square(s, (0,) if last else both)
-            if ahead < NPAIR:
-                copy_x(ahead, 0)
-            if 0 <= s - 1:
-                copy_n(s - 1, both)
-            if last:
-                find_rstd(s, (0,))
-                square(s, (1,))
-                scale_n(s, (0,))
-                find_rstd(s, (1,))
-                scale_n(s, (1,))
-            else:
-                find_rstd(s, both)
-                if ahead < NPAIR:
-                    copy_x(ahead, 1)
-                scale_n(s, both)
-            if s > 0 and s + 1 < NPAIR:
+            if s >= 2:
+                quantise_n(s - 2)
+            if live:
+                down(s)
+            if s >= 2:
+                up(s - 2)
+            if live:
+                add_bias_l(s)
+            if 2 <= s + 1 < NPAIR:
                 quantise_x(s + 1)
+            if live:
+                add_bias_r(s)
+                rotate(s)
+            if s + 2 < NPAIR:
+                turn_x(s + 2)
+            if 1 <= s <= NPAIR:
+                turn_n(s - 1)
+            if live:
+                square(s)
+            if s + 2 < NPAIR:
+                copy_x(s + 2, 0)
+            if 1 <= s <= NPAIR:
+                copy_n(s - 1)
+            if live:
+                find_rstd(s)
+            if s + 2 < NPAIR:
+                copy_x(s + 2, 1)
+            if live:
+                scale_n(s)
             if s < 2:
                 regroup_wu(256 * s, 256 * s + 256)
             if s == 1:
                 quantise_wu()
-                spread_bias(nc.scalar.copy, ps_kv, "kv", 640, 1152)
-            if 0 <= s - 2:
+                spread_bias(nc.scalar.copy, 640, 1152)
+            if s >= 2:
                 spread_heads(s - 2)
-                finish(s - 2, both)
-                store(s - 2, both)
-        i = NPAIR - 1
-        quantise_n(i - 1, both)
-        up(i - 1, both)
-        for a in both:
-            turn_n(i, (a,))
-            copy_n(i, (a,))
-        spread_heads(i - 1)
-        finish(i - 1, both)
-        store(i - 1, both)
-        spread_heads(i)
-        for a in both:
-            quantise_n(i, (a,))
-            up(i, (a,))
-            finish(i, (a,))
-            store(i, (a,))
+                finish(s - 2)
+                store(s - 2)

@@ -386,11 +386,11 @@ def tile_mla_pb_t_kernel(tc, X, Wkv_down, bkv_down, Wkv_up, bkv_up, out_0, out_1
         regroup_wd(nc.vector.tensor_copy, 1, 0, 128)
         quantise_wd(0, 0, 128)
         quantise_wd(1, 0, 128)
+        regroup_wu(0, 512)
         turn_x(1)
         copy_x(1, 0)
         copy_x(1, 1)
         finish_tables()
-        quantise_x(1)
         open_x(6)
         load_x(6, 0, 4)
         for s in range(NPAIR + 2):
@@ -406,7 +406,7 @@ def tile_mla_pb_t_kernel(tc, X, Wkv_down, bkv_down, Wkv_up, bkv_up, out_0, out_1
                 up(s - 2)
             if live:
                 add_bias_l(s)
-            if 2 <= s + 1 < NPAIR:
+            if s + 1 < NPAIR:
                 quantise_x(s + 1)
             if live:
                 add_bias_r(s)
@@ -427,9 +427,7 @@ def tile_mla_pb_t_kernel(tc, X, Wkv_down, bkv_down, Wkv_up, bkv_up, out_0, out_1
                 copy_x(s + 2, 1)
             if live:
                 scale_n(s)
-            if s < 2:
-                regroup_wu(256 * s, 256 * s + 256)
-            if s == 1:
+            if s == 0:
                 quantise_wu()
                 spread_bias(nc.scalar.copy, 640, 1152)
             if s >= 2:

from contextlib import ExitStack
import math

import concourse.mybir as mybir
from concourse.masks import make_identity

FLOPS = 2 * 4096 * (1024 * 640 + 512 * 512)

F32 = mybir.dt.float32
BF16 = mybir.dt.bfloat16
U32 = mybir.dt.uint32
U8 = mybir.dt.uint8
I32 = mybir.dt.int32
FP8X4 = mybir.dt.float8_e4m3fn_x4
AF = mybir.ActivationFunctionType
ALU = mybir.AluOpType

P = 128
NQUAD = 8
NXBUF = 6
NPAIR = 16
EPS = 1e-6
TWO_PI = 2.0 * math.pi


def tile_mla_pb_t_kernel(tc, X, Wkv_down, bkv_down, Wkv_up, bkv_up, out_0, out_1):
    nc = tc.nc
    with ExitStack() as ctx:
        const = ctx.enter_context(tc.tile_pool(name="const", bufs=1))
        xres = ctx.enter_context(tc.tile_pool(name="xres", bufs=NXBUF))
        xg_pool = ctx.enter_context(tc.tile_pool(name="xg", bufs=4))
        l_pool = ctx.enter_context(tc.tile_pool(name="lp", bufs=6))
        n_pool = ctx.enter_context(tc.tile_pool(name="np", bufs=4))
        small = ctx.enter_context(tc.tile_pool(name="small", bufs=4))
        rope = ctx.enter_context(tc.tile_pool(name="rope", bufs=2))
        rkeep = ctx.enter_context(tc.tile_pool(name="rkeep", bufs=4))
        outp = ctx.enter_context(tc.tile_pool(name="outp", bufs=3))
        ps_xt = ctx.enter_context(tc.psum_pool(name="ps_xt", bufs=2))
        ps_l = ctx.enter_context(tc.psum_pool(name="ps_l", bufs=2))
        ps_r = ctx.enter_context(tc.psum_pool(name="ps_r", bufs=1))
        ps_nt = ctx.enter_context(tc.psum_pool(name="ps_nt", bufs=1))
        ps_kv = ctx.enter_context(tc.psum_pool(name="ps_kv", bufs=2))

        ctx.enter_context(tc.manual_schedule())

        wd_raw = const.tile([P, 2, 4, 640], BF16, name="wd_raw")
        wd_src = Wkv_down.rearrange("(a q e) c -> q a (e c)", a=4, q=P, e=2)
        wd_dst = wd_raw[:].rearrange("q g (u e) c -> q (g u) (e c)", u=2, e=2)
        wu_raw = const.tile([P, 4, 512], BF16, name="wu_raw")
        x_sb = []

        def open_x(G):
            x_sb.append(xres.tile([P, 4096], BF16, name="x_sb"))

        def load_x(G, lo, hi):
            b, g = divmod(G, 2)
            src = X[b, g * 512 : (g + 1) * 512, :].rearrange("(p t) k -> p t k", t=4)
            dst = x_sb[G][:].rearrange("p (t k) -> p t k", t=4)
            nc.sync.dma_start(out=dst[:, lo:hi, :], in_=src[:, lo:hi, :])

        brow = const.tile([P, 1152], BF16, name="brow")
        nc.vector.memset(brow[:].bitcast(I32), 0)
        open_x(0)
        load_x(0, 0, 1)
        load_x(0, 1, 2)
        nc.sync.dma_start(out=wd_dst[:, 0:2, :], in_=wd_src[:, 0:2, :])
        nc.sync.dma_start(out=wd_dst[:, 2:4, :], in_=wd_src[:, 2:4, :])
        nc.sync.dma_start(out=brow[0:1, 0:640], in_=bkv_down.rearrange("(o n) -> o n", o=1))
        nc.sync.dma_start(out=brow[0:1, 640:1152], in_=bkv_up.rearrange("(o n) -> o n", o=1))
        load_x(0, 2, 4)
        nc.sync.dma_start(
            out=wu_raw[:].rearrange("p (u e) n -> p u (e n)", u=2),
            in_=Wkv_up.rearrange("(u p e) n -> p u (e n)", u=2, p=P, e=2),
        )
        for G in range(1, NXBUF):
            open_x(G)
            load_x(G, 0, 4)

        ones = const.tile([P, P], BF16, name="ones")
        nc.vector.memset(ones[:], 1.0)
        eps_t = const.tile([P, 1], F32, name="eps_t")
        nc.vector.memset(eps_t[:], 0.0)
        nc.vector.tensor_scalar_add(out=eps_t[:], in0=eps_t[:], scalar1=EPS)

        warm = const.tile([P, 2], F32, name="warm")
        nc.scalar.activation(out=warm[:, 0:1], in_=eps_t[:], func=AF.Sin)

        ident_f = const.tile([P, P], F32, name="ident_f")
        make_identity(nc, ident_f[:])

        pos = const.tile([P, 8], F32, name="pos")
        nc.gpsimd.iota(
            pos[:],
            pattern=[[512, 2], [1, 4]],
            base=0,
            channel_multiplier=4,
            allow_small_or_imprecise_dtypes=True,
        )
        rows = const.tile([P, 2, 8], F32, name="rows")
        nc.vector.memset(rows[:, :, 0:1], 1.0)
        nc.vector.tensor_scalar_mul(out=rows[:, 0, 0:1], in0=rows[:, 0, 0:1], scalar1=1.0 / TWO_PI)
        ratio = 10000.0 ** (-1.0 / 64.0)
        for n in (1, 2, 4):
            for k, step in ((1, 1), (0, 8)):
                nc.vector.tensor_scalar_mul(
                    out=rows[:, k, n : 2 * n], in0=rows[:, k, 0:n], scalar1=ratio ** (n * step)
                )
        tf = const.tile([P, 8, 8], F32, name="tf")
        nc.vector.tensor_tensor(
            out=tf[:],
            in0=rows[:, 0].unsqueeze(2).to_broadcast([P, 8, 8]),
            in1=rows[:, 1].unsqueeze(1).to_broadcast([P, 8, 8]),
            op=ALU.mult,
        )
        turns = const.tile([P, 8, 64], F32, name="turns")
        nc.vector.tensor_tensor(
            out=turns[:],
            in0=pos[:].unsqueeze(2).to_broadcast([P, 8, 64]),
            in1=tf[:].rearrange("p a b -> p (a b)").unsqueeze(1).to_broadcast([P, 8, 64]),
            op=ALU.mult,
        )

        def g_scale(out, in_, factor, offset=0.0):
            nc.gpsimd.tensor_scalar(out=out, in0=in_, scalar1=factor, scalar2=offset, op0=ALU.mult, op1=ALU.add)

        whole = const.tile([P, 8, 64], I32, name="whole")
        frac = const.tile([P, 8, 64], F32, name="frac")
        half_sin = const.tile([P, 8, 64], F32, name="half_sin")
        table = const.tile([P, 2, 8, 2, 64], F32, name="table")

        nc.vector.tensor_copy(out=whole[:], in_=turns[:])
        nc.vector.tensor_tensor(out=frac[:], in0=turns[:], in1=whole[:], op=ALU.subtract)

        def find_sines():
            nc.scalar.activation(out=half_sin[:], in_=frac[:], func=AF.Sin, scale=0.5 * TWO_PI)
            nc.scalar.activation(out=table[:, 1, :, 0, :], in_=frac[:], func=AF.Sin, scale=TWO_PI)

        def finish_tables():
            nc.scalar.activation(out=half_sin[:], in_=half_sin[:], func=AF.Square)
            g_scale(table[:, 0, :, 0, :], half_sin[:], -2.0, 1.0)
            g_scale(table[:, 0, :, 1, :], half_sin[:], -2.0, 1.0)
            g_scale(table[:, 1, :, 1, :], table[:, 1, :, 0, :], -1.0)

        bias_sb = const.tile([P, 1152], F32, name="bias_sb")

        def spread_bias(eng_copy, lo, hi):
            bps = ps_kv.tile([P, 512], F32, name="bps", tag="kv")
            nc.tensor.matmul(bps[:, 0 : hi - lo], lhsT=ones[:], rhs=brow[:, lo:hi], start=True, stop=True)
            eng_copy(out=bias_sb[:, lo:hi], in_=bps[:, 0 : hi - lo])

        wdg = const.tile([P, 2, 640, 4], BF16, name="wdg", align_bytes=64)
        wdc = const.tile([P, 2, 640], U32, name="wdc", align_bytes=64)
        wds = const.tile([P, 2, 640], U8, name="wds", align_bytes=64)

        def regroup_wd(eng_copy, g, lo, hi):
            eng_copy(
                out=wdg[:, g, lo:hi, :].rearrange("q (c i) j -> q c j i", i=4),
                in_=wd_raw[:, g, :, lo:hi].rearrange("q j (c i) -> q c j i", i=4),
            )

        def quantise_wd(g, lo, hi):
            nc.vector.quantize_mx(
                out=wdc[:, g, lo:hi].bitcast(FP8X4),
                scales=wds[:, g, lo:hi],
                in_=wdg[:, g, lo:hi, :].rearrange("q c j -> q (c j)"),
            )

        wug = const.tile([P, 512, 4], BF16, name="wug", align_bytes=64)
        wuc = const.tile([P, 512], U32, name="wuc", align_bytes=64)
        wus = const.tile([P, 512], U8, name="wus", align_bytes=64)

        def regroup_wu(lo, hi):
            nc.vector.tensor_copy(
                out=wug[:, lo:hi].rearrange("q (c i) j -> q c j i", i=4),
                in_=wu_raw[:, :, lo:hi].rearrange("q j (c i) -> q c j i", i=4),
            )

        def quantise_wu():
            nc.vector.quantize_mx(
                out=wuc[:].bitcast(FP8X4), scales=wus[:], in_=wug[:].rearrange("q c j -> q (c j)")
            )

        st = {}

        def turn_x(i):
            G, half = divmod(i, 2)
            xw = x_sb[G][:].bitcast(F32)
            xts = []
            for a in range(2):
                t = 2 * half + a
                xt = ps_xt.tile([P, 4, P], F32, name="xt")
                for j in range(4):
                    c0 = t * 512 + j * P
                    nc.tensor.transpose(xt[:, j, :], xw[:, c0 : c0 + P], ident_f[:])
                xts.append(xt)
            st[("xt", i)] = xts

        def copy_x(i, a):
            if a == 0:
                st[("xg", i)] = xg_pool.tile([P, 2048], BF16, name="xg", align_bytes=64)
            xgw = st[("xg", i)][:].bitcast(F32)
            nc.scalar.copy(
                out=xgw[:, a * 512 : (a + 1) * 512].rearrange("q (g t u) -> q g t u", g=2, t=P, u=2),
                in_=st[("xt", i)][a][:].rearrange("q (g u) t -> q g t u", g=2, u=2),
            )

        def quantise_x(i):
            xg = st.pop(("xg", i))
            xc = xg_pool.tile([P, 512], U32, name="xc", align_bytes=64)
            xs = xg_pool.tile([P, 512], U8, name="xs", align_bytes=64)
            nc.vector.quantize_mx(out=xc[:].bitcast(FP8X4), scales=xs[:], in_=xg[:])
            st[("x", i)] = (xc, xs)

        def down(i):
            xc, xs = st.pop(("x", i))
            r_ps = ps_r.tile([P, 2, P], F32, name="r_ps")
            l_pss = [ps_l.tile([P, 512], F32, name="l_ps") for a in range(2)]
            outs = [(a, l_pss[a][:], 128, 640) for a in range(2)] + [(a, r_ps[:, a, :], 0, 128) for a in range(2)]
            for a, out, lo, hi in outs:
                for g in range(2):
                    o = a * 256 + g * P
                    nc.tensor.matmul_mx(
                        out=out,
                        lhsT=xc[:, o : o + P].bitcast(FP8X4),
                        lhsT_scale=xs[:, o : o + P],
                        rhs=wdc[:, g, lo:hi].bitcast(FP8X4),
                        rhs_scale=wds[:, g, lo:hi],
                        start=(g == 0),
                        stop=(g == 1),
                    )
            st[("d", i)] = (l_pss, r_ps)

        def add_bias_l(i):
            st[("l", i)] = []
            for l_ps in st[("d", i)][0]:
                l_sb = l_pool.tile([P, 512], F32, name="l_sb")
                nc.vector.tensor_tensor(out=l_sb[:], in0=l_ps[:], in1=bias_sb[:, 128:640], op=ALU.add)
                st[("l", i)].append(l_sb)

        def add_bias_r(i):
            r_ps = st.pop(("d", i))[1]
            r_sb = rkeep.tile([P, 2, P], F32, name="r_sb")
            nc.vector.tensor_tensor(
                out=r_sb[:],
                in0=r_ps[:],
                in1=bias_sb[:, 0:128].unsqueeze(1).to_broadcast([P, 2, P]),
                op=ALU.add,
            )
            st[("r", i)] = r_sb

        def square(i):
            ss = small.tile([P, 2], F32, name="ss")
            for a in range(2):
                junk = small.tile([P, 512], BF16, name="junk")
                nc.scalar.activation(
                    out=junk[:], in_=st[("l", i)][a][:], func=AF.Square, accum_out=ss[:, a : a + 1]
                )
            st[("ss", i)] = ss

        def find_rstd(i):
            rstd = small.tile([P, 2], F32, name="rstd")
            nc.scalar.activation(
                out=rstd[:],
                in_=st.pop(("ss", i))[:],
                func=AF.Abs_reciprocal_sqrt,
                scale=1.0 / 512.0,
                bias=eps_t[:, 0:1],
            )
            st[("s", i)] = rstd

        def scale_n(i):
            l_sbs = st.pop(("l", i))
            rstd = st.pop(("s", i))
            n_bf = n_pool.tile([P, 2, 512], BF16, name="n_bf")
            for a in range(2):
                nc.scalar.activation(out=n_bf[:, a, :], in_=l_sbs[a][:], func=AF.Copy, scale=rstd[:, a : a + 1])
            st[("n", i)] = n_bf

        def rotate(i):
            G, half = divmod(i, 2)
            r_sb = st.pop(("r", i))
            if half == 0:
                key_sb = outp.tile([P, 4, 4, 192], F32, name="key_sb")
                val_sb = outp.tile([P, 4, 4, 64], F32, name="val_sb")
                st[("o", G)] = (key_sb, val_sb)
            key_sb, val_sb = st[("o", G)]
            t0 = 2 * half
            gt = (G % 2) * 4 + t0
            both = rope.tile([P, 2, 2, 2, 64], F32, name="both")
            fl = "p x a h d -> p x (a h d)"
            nc.gpsimd.tensor_tensor(
                out=both[:].rearrange(fl),
                in0=r_sb[:].rearrange("p a c -> p (a c)").unsqueeze(1).to_broadcast([P, 2, 2 * P]),
                in1=table[:, :, gt : gt + 2].rearrange(fl),
                op=ALU.mult,
            )
            nc.gpsimd.tensor_tensor(
                out=key_sb[:, 0, t0 : t0 + 2, 64:192].rearrange("p a (h d) -> p a h d", h=2),
                in0=both[:, 0],
                in1=both[:, 1, :, ::-1, :],
                op=ALU.add,
            )

        def spread_heads(i):
            G, half = divmod(i, 2)
            rope_cols = st[("o", G)][0][:, :, 2 * half : 2 * half + 2, 64:192]
            nc.vector.tensor_copy(out=rope_cols[:, 1:4], in_=rope_cols[:, 0:1].to_broadcast([P, 3, 2, P]))

        def turn_n(i):
            nw = st.pop(("n", i))[:].rearrange("p a c -> p (a c)").bitcast(F32)
            nt = ps_nt.tile([P, 2, 2, P], F32, name="nt")
            for a in range(2):
                for u in range(2):
                    c0 = a * 256 + u * P
                    nc.tensor.transpose(nt[:, a, u, :], nw[:, c0 : c0 + P], ident_f[:])
            st[("nt", i)] = nt

        def copy_n(i):
            ng = n_pool.tile([P, 1024], BF16, name="ng", align_bytes=64)
            nc.scalar.copy(
                out=ng[:].bitcast(F32).rearrange("p (a t u) -> p a t u", a=2, t=P, u=2),
                in_=st.pop(("nt", i))[:].rearrange("p a u t -> p a t u"),
            )
            st[("ng", i)] = ng

        def quantise_n(i):
            ncd = n_pool.tile([P, 256], U32, name="ncd", align_bytes=64)
            nsc = n_pool.tile([P, 256], U8, name="nsc", align_bytes=64)
            nc.vector.quantize_mx(out=ncd[:].bitcast(FP8X4), scales=nsc[:], in_=st.pop(("ng", i))[:])
            st[("q", i)] = (ncd, nsc)

        def up(i):
            ncd, nsc = st.pop(("q", i))
            kvs = []
            for a in range(2):
                kv = ps_kv.tile([P, 512], F32, name="kv")
                nc.tensor.matmul_mx(
                    out=kv[:],
                    lhsT=ncd[:, a * P : (a + 1) * P].bitcast(FP8X4),
                    lhsT_scale=nsc[:, a * P : (a + 1) * P],
                    rhs=wuc[:].bitcast(FP8X4),
                    rhs_scale=wus[:],
                    start=True,
                    stop=True,
                )
                kvs.append(kv)
            st[("u", i)] = kvs

        def finish(i):
            G, half = divmod(i, 2)
            key_sb, val_sb = st[("o", G)]
            buv = bias_sb[:, 640:1152].rearrange("p (h x d) -> p h x d", h=4, x=2, d=64)
            for a, kv in enumerate(st.pop(("u", i))):
                t = 2 * half + a
                kvv = kv[:].rearrange("p (h x d) -> p h x d", h=4, x=2, d=64)
                nc.vector.tensor_tensor(out=key_sb[:, :, t, 0:64], in0=kvv[:, :, 0, :], in1=buv[:, :, 0, :], op=ALU.add)
                nc.vector.tensor_tensor(out=val_sb[:, :, t, :], in0=kvv[:, :, 1, :], in1=buv[:, :, 1, :], op=ALU.add)

        def store(i):
            G, half = divmod(i, 2)
            key_sb, val_sb = st[("o", G)]
            b, g = divmod(G, 2)
            lo, hi = 2 * half, 2 * half + 2
            for out, sb in ((out_0, key_sb), (out_1, val_sb)):
                nc.sync.dma_start(
                    out=out[b].rearrange("h (g p t) d -> g p h t d", g=2, p=P, t=4)[g][:, :, lo:hi, :],
                    in_=sb[:, :, lo:hi, :],
                )

        vsplit = 128 + 384
        turn_x(0)
        copy_x(0, 0)
        copy_x(0, 1)
        find_sines()
        regroup_wd(nc.vector.tensor_copy, 0, 128, vsplit)
        regroup_wd(nc.scalar.copy, 0, vsplit, 640)
        quantise_x(0)
        regroup_wd(nc.vector.tensor_copy, 1, 128, vsplit)
        regroup_wd(nc.scalar.copy, 1, vsplit, 640)
        nc.scalar.activation(out=warm[:, 1:2], in_=eps_t[:], func=AF.Abs_reciprocal_sqrt, bias=eps_t[:])
        quantise_wd(0, 128, 640)
        quantise_wd(1, 128, 640)
        spread_bias(nc.scalar.copy, 128, 640)
        spread_bias(nc.scalar.copy, 0, 128)
        regroup_wd(nc.vector.tensor_copy, 0, 0, 128)
        regroup_wd(nc.vector.tensor_copy, 1, 0, 128)
        quantise_wd(0, 0, 128)
        quantise_wd(1, 0, 128)
        regroup_wu(0, 512)
        turn_x(1)
        copy_x(1, 0)
        copy_x(1, 1)
        finish_tables()
        open_x(6)
        load_x(6, 0, 4)
        for s in range(NPAIR + 2):
            live = s < NPAIR
            if s == 2:
                open_x(7)
                load_x(7, 0, 4)
            if s >= 2:
                quantise_n(s - 2)
            if live:
                down(s)
            if s >= 2:
                up(s - 2)
            if live:
                add_bias_l(s)
            if s + 1 < NPAIR:
                quantise_x(s + 1)
            if live:
                add_bias_r(s)
                rotate(s)
            if s + 2 < NPAIR:
                turn_x(s + 2)
            if 1 <= s <= NPAIR:
                turn_n(s - 1)
            if live:
                square(s)
            if s + 2 < NPAIR:
                copy_x(s + 2, 0)
            if 1 <= s <= NPAIR:
                copy_n(s - 1)
            if live:
                find_rstd(s)
            if s + 2 < NPAIR:
                copy_x(s + 2, 1)
            if live:
                scale_n(s)
            if s == 0:
                quantise_wu()
                spread_bias(nc.scalar.copy, 640, 1152)
            if s >= 2:
                spread_heads(s - 2)
                finish(s - 2)
                store(s - 2)
